import numpy as np
import ml_dtypes


def mxq(x, axis, fmt="e4m3"):
    dtype, down = {"e4m3": (ml_dtypes.float8_e4m3fn, 7), "e5m2": (ml_dtypes.float8_e5m2, 14)}[fmt]
    v = np.moveaxis(np.asarray(x, np.float32).astype(ml_dtypes.bfloat16).astype(np.float64), axis, -1)
    blocks = v.reshape(v.shape[:-1] + (-1, 32))
    amax = np.abs(blocks).max(-1, keepdims=True)
    byte = np.maximum(np.where(amax > 0, np.frexp(amax)[1] - 1 + 127, 0) - down, 1)
    scale = np.exp2(byte - 127.0)
    codes = (blocks / scale).astype(np.float32).astype(dtype).astype(np.float64)
    return np.moveaxis((codes * scale).reshape(v.shape), -1, axis)


WIDE = False


def mx_kscale(k):
    if not WIDE:
        return np.ones(k)
    levels = np.array([10, -10, 5, -5, 0])
    a = np.random.permutation(np.resize(levels, k // 512 * 4)).reshape(k // 512, 4)
    idx = np.arange(k)
    return np.exp2(a[idx // 512, idx % 128 // 32])


BF16 = ml_dtypes.bfloat16


def bf(x):
    return np.asarray(x, np.float32).astype(BF16)


def f64(x):
    return np.asarray(x).astype(np.float64)


B, S, D, H, QK = 1, 1024, 1024, 2048, 128
R = np.sqrt(0.1 * S / np.sqrt(QK))


def silu(a):
    return a / (1.0 + np.exp(-a))


def setup_inputs():
    u = np.exp2(np.round(np.log2(mx_kscale(S)) / 2))
    t = mx_kscale(H)
    return {
        "q": bf(np.random.standard_normal((B, S, QK)) * R),
        "k": bf(np.random.standard_normal((B, S, QK)) * R * u[:, None]),
        "v": bf(silu(np.random.standard_normal((B, S, H))) / (u * u)[:, None]),
        "gate": bf(silu(np.random.standard_normal((B, S, H))) * t),
        "W_out": bf(np.random.standard_normal((D, H)) / np.sqrt(H) / t),
        "b_out": bf(np.random.standard_normal(D) * 0.1),
        "x": bf(np.random.standard_normal((B, S, D))),
    }


def reference(q, k, v, gate, W_out, b_out, x):
    sim = f64(q) @ f64(k).transpose(0, 2, 1) / S
    A = np.square(np.maximum(sim, 0.0))
    V = (mxq(A, 2, "e4m3") @ mxq(f64(v), 1, "e4m3")) * f64(gate)
    return (mxq(V, 2, "e4m3") @ mxq(f64(W_out), 1, "e4m3").T) + f64(b_out) + f64(x)

@@ -1,0 +1,243 @@
+from contextlib import ExitStack
+
+import concourse.mybir as mybir
+from concourse.masks import make_identity
+
+BF16 = mybir.dt.bfloat16
+F32 = mybir.dt.float32
+U32 = mybir.dt.uint32
+U8 = mybir.dt.uint8
+FP8X4 = mybir.dt.float8_e4m3fn_x4
+ACT = mybir.ActivationFunctionType
+ALU = mybir.AluOpType
+
+P = 128
+PACK = 4
+K_PASS = P * PACK
+S = 1024
+QK = 128
+H = 2048
+D = 1024
+TOKEN_BLOCKS = S // P
+KEY_PASSES = S // K_PASS
+HID_PASSES = H // K_PASS
+D_HALF = 512
+RAW_BUFS = 5
+
+FLOPS = 2 * S * S * QK + 2 * S * S * H + 2 * S * H * D
+
+
+def tile_gau_pa_kernel(tc, q, k, v, gate, W_out, b_out, x, out):
+    nc = tc.nc
+    q_rows = q.flatten_outer_dims()
+    k_rows = k.flatten_outer_dims()
+    v_rows = v.flatten_outer_dims()
+    gate_rows = gate.flatten_outer_dims()
+    x_rows = x.flatten_outer_dims().rearrange("(p a) d -> p a d", a=TOKEN_BLOCKS)
+    out_rows = out.flatten_outer_dims().rearrange("(p a) d -> p a d", a=TOKEN_BLOCKS)
+
+    with ExitStack() as ctx:
+        keep = ctx.enter_context(tc.tile_pool(name="keep", bufs=1))
+        raw_pool = ctx.enter_context(tc.tile_pool(name="raw", bufs=RAW_BUFS))
+        grp_pool = ctx.enter_context(tc.tile_pool(name="grp", bufs=2))
+        work = ctx.enter_context(tc.tile_pool(name="work", bufs=2))
+        psum_tp = ctx.enter_context(tc.psum_pool(name="psum_tp", bufs=2))
+        psum_s1 = ctx.enter_context(tc.psum_pool(name="psum_s1", bufs=3))
+        psum_s2 = ctx.enter_context(tc.psum_pool(name="psum_s2", bufs=3))
+
+        k_sb = keep.tile([P, KEY_PASSES * PACK, QK], BF16, name="k_sb")
+        nc.sync.dma_start(
+            out=k_sb[:].rearrange("p (c t) d -> p c t d", c=KEY_PASSES),
+            in_=k_rows.rearrange("(c p t) d -> p c t d", c=KEY_PASSES, t=PACK),
+        )
+        q_sb = keep.tile([P, TOKEN_BLOCKS, QK], BF16, name="q_sb")
+        nc.sync.dma_start(out=q_sb[:], in_=q_rows.rearrange("(p a) d -> p a d", a=TOKEN_BLOCKS))
+
+        v_raw = []
+        for g in range(HID_PASSES):
+            raw = raw_pool.tile([P, KEY_PASSES * PACK * K_PASS], BF16, name="v_raw%d" % g, tag="raw")
+            raw_view = raw[:].rearrange("p (c t h) -> p c t h", c=KEY_PASSES, t=PACK)
+            for c in range(KEY_PASSES):
+                nc.sync.dma_start(
+                    out=raw_view[:, c, :, :],
+                    in_=v_rows[K_PASS * c : K_PASS * (c + 1), K_PASS * g : K_PASS * (g + 1)].rearrange(
+                        "(p t) h -> p t h", t=PACK
+                    ),
+                )
+            v_raw.append(raw)
+        gate_raw = []
+        for g in range(HID_PASSES):
+            raw = raw_pool.tile([P, TOKEN_BLOCKS * K_PASS], BF16, name="gate_raw%d" % g, tag="raw")
+            nc.sync.dma_start(
+                out=raw[:].rearrange("p (a h) -> p a h", a=TOKEN_BLOCKS),
+                in_=gate_rows[:, K_PASS * g : K_PASS * (g + 1)].rearrange("(p a) h -> p a h", a=TOKEN_BLOCKS),
+            )
+            gate_raw.append(raw)
+        w_raw = []
+        for g in range(HID_PASSES):
+            raw = raw_pool.tile([P, (D // P) * K_PASS], BF16, name="w_raw%d" % g, tag="raw")
+            nc.sync.dma_start(
+                out=raw[:].rearrange("p (a h) -> p a h", a=D // P),
+                in_=W_out[:, K_PASS * g : K_PASS * (g + 1)].rearrange("(a p) h -> p a h", p=P),
+            )
+            w_raw.append(raw)
+        bias_all = keep.tile([P, D], BF16, name="bias_all")
+        nc.sync.dma_start(out=bias_all[:], in_=b_out.partition_broadcast(P))
+        x_raw = []
+        for xh in range(2):
+            raw = raw_pool.tile([P, 4 * D], BF16, name="x_raw%d" % xh, tag="raw")
+            nc.sync.dma_start(
+                out=raw[:].rearrange("p (a d) -> p a d", a=4),
+                in_=x_rows[:, 4 * xh : 4 * xh + 4, :],
+            )
+            x_raw.append(raw)
+
+        ident_bf = keep.tile([P, P], BF16, name="ident_bf")
+        make_identity(nc, ident_bf[:])
+        ident_f32 = keep.tile([P, P], F32, name="ident_f32")
+        make_identity(nc, ident_f32[:])
+
+        kT = keep.tile([P, KEY_PASSES * PACK, P], BF16, name="kT")
+        qT = keep.tile([P, TOKEN_BLOCKS, P], BF16, name="qT")
+        a_codes = keep.tile([P, TOKEN_BLOCKS, KEY_PASSES * P], U32, name="a_codes", align_bytes=64)
+        a_scales = keep.tile([P, TOKEN_BLOCKS, KEY_PASSES * P], U8, name="a_scales", align_bytes=64)
+        v_codes = keep.tile([P, HID_PASSES, KEY_PASSES * K_PASS], U32, name="v_codes", align_bytes=64)
+        v_scales = keep.tile([P, HID_PASSES, KEY_PASSES * K_PASS], U8, name="v_scales", align_bytes=64)
+        w_codes = keep.tile([P, HID_PASSES, D], U32, name="w_codes", align_bytes=64)
+        w_scales = keep.tile([P, HID_PASSES, D], U8, name="w_scales", align_bytes=64)
+        g_codes = keep.tile([P, HID_PASSES, S], U32, name="g_codes", align_bytes=64)
+        g_scales = keep.tile([P, HID_PASSES, S], U8, name="g_scales", align_bytes=64)
+        gateT = []
+        for g in range(HID_PASSES):
+            gateT_g = keep.tile([P, S * PACK], BF16, name="gateT%d" % g)
+            gateT.append(gateT_g)
+        resid = keep.tile([P, TOKEN_BLOCKS, D], F32, name="resid")
+
+        for src, dst in ((k_sb, kT), (q_sb, qT)):
+            for half in range(2):
+                tp = psum_tp.tile([P, 4, P], BF16, name="tp_qk", tag="tp")
+                for n in range(4):
+                    nc.tensor.transpose(tp[:, n, :], src[:, 4 * half + n, :], ident_bf[:])
+                nc.vector.tensor_copy(out=dst[:, 4 * half : 4 * half + 4, :], in_=tp[:])
+
+        def prepare_scores(a):
+            relu_sim = work.tile([P, KEY_PASSES, P, PACK], F32, name="relu_sim", tag="relu_sim")
+            for c in range(KEY_PASSES):
+                sim = psum_s1.tile([P, PACK, P], F32, name="sim", tag="s1")
+                for t in range(PACK):
+                    nc.tensor.matmul(
+                        out=sim[:, t, :], lhsT=kT[:, PACK * c + t, :], rhs=qT[:, a, :], start=True, stop=True
+                    )
+                nc.scalar.activation(
+                    out=relu_sim[:, c, :, :],
+                    in_=sim[:].rearrange("p t i -> p i t"),
+                    func=ACT.Relu,
+                    scale=1.0 / S,
+                )
+            a_grp = work.tile([P, KEY_PASSES * P * PACK], BF16, name="a_grp", tag="a_grp", align_bytes=64)
+            nc.scalar.activation(
+                out=a_grp[:], in_=relu_sim[:].rearrange("p c i t -> p (c i t)"), func=ACT.Square
+            )
+            nc.vector.quantize_mx(out=a_codes[:, a, :].bitcast(FP8X4), scales=a_scales[:, a, :], in_=a_grp[:])
+
+        def prepare_values(g):
+            src = v_raw[g][:].rearrange(
+                "p (c t u m e) -> p c u e m t", c=KEY_PASSES, t=PACK, u=2, e=2
+            )
+            v_grp = grp_pool.tile([P, KEY_PASSES * K_PASS * PACK], BF16, name="v_grp", tag="grp", align_bytes=64)
+            dst = v_grp[:].rearrange("p (c u e m t) -> p c u e m t", c=KEY_PASSES, u=2, e=2, t=PACK)
+            for c in range(KEY_PASSES):
+                nc.vector.tensor_copy(out=dst[:, c, :, :, :, :], in_=src[:, c, :, :, :, :])
+            nc.vector.quantize_mx(out=v_codes[:, g, :].bitcast(FP8X4), scales=v_scales[:, g, :], in_=v_grp[:])
+
+        def transpose_words(raw, dst_words):
+            words = raw[:].bitcast(F32)
+            for pair in range(4):
+                tp = psum_tp.tile([P, 2, 2, P], F32, name="tp_w", tag="tp")
+                for n in range(2):
+                    for u in range(2):
+                        first = 256 * (2 * pair + n) + P * u
+                        nc.tensor.transpose(tp[:, n, u, :], words[:, first : first + P], ident_f32[:])
+                nc.scalar.copy(
+                    out=dst_words[:, 2 * pair : 2 * pair + 2, :, :], in_=tp[:].rearrange("p n u r -> p n r u")
+                )
+
+        def prepare_gate(g):
+            transpose_words(
+                gate_raw[g], gateT[g][:].bitcast(F32).rearrange("p (a r u) -> p a r u", a=TOKEN_BLOCKS, u=2)
+            )
+
+        def prepare_weights(g):
+            w_grp = grp_pool.tile([P, D * PACK], BF16, name="w_grp", tag="grp", align_bytes=64)
+            transpose_words(w_raw[g], w_grp[:].bitcast(F32).rearrange("p (a r u) -> p a r u", a=D // P, u=2))
+            nc.vector.quantize_mx(out=w_codes[:, g, :].bitcast(FP8X4), scales=w_scales[:, g, :], in_=w_grp[:])
+
+        def attend(g, half):
+            gate_view = gateT[g][:].rearrange("p (a i t) -> p a i t", a=TOKEN_BLOCKS, t=PACK)
+            gated = work.tile([P, 4, P, PACK], BF16, name="gated", tag="gated", align_bytes=64)
+            for n in range(4):
+                a = 4 * half + n
+                av = psum_s1.tile([P, PACK, P], F32, name="av", tag="s1")
+                for t in range(PACK):
+                    for c in range(KEY_PASSES):
+                        v_cols = slice(K_PASS * c + P * t, K_PASS * c + P * (t + 1))
+                        a_cols = slice(P * c, P * (c + 1))
+                        nc.tensor.matmul_mx(
+                            out=av[:, t, :],
+                            lhsT=v_codes[:, g, v_cols].bitcast(FP8X4),
+                            lhsT_scale=v_scales[:, g, v_cols],
+                            rhs=a_codes[:, a, a_cols].bitcast(FP8X4),
+                            rhs_scale=a_scales[:, a, a_cols],
+                            start=(c == 0),
+                            stop=(c == KEY_PASSES - 1),
+                        )
+                nc.vector.tensor_tensor(
+                    out=gated[:, n, :, :],
+                    in0=av[:].rearrange("p t i -> p i t"),
+                    in1=gate_view[:, a, :, :],
+                    op=ALU.mult,
+                )
+            cols = slice(4 * P * half, 4 * P * (half + 1))
+            nc.vector.quantize_mx(
+                out=g_codes[:, g, cols].bitcast(FP8X4),
+                scales=g_scales[:, g, cols],
+                in_=gated[:].rearrange("p n i t -> p (n i t)"),
+            )
+
+        def prepare_residual(a):
+            x_view = x_raw[a // 4][:].rearrange("p (a d) -> p a d", a=4)
+            nc.gpsimd.tensor_tensor(out=resid[:, a, :], in0=x_view[:, a % 4, :], in1=bias_all[:], op=ALU.add)
+
+        def project(a):
+            for dh in range(D // D_HALF):
+                d_cols = slice(D_HALF * dh, D_HALF * (dh + 1))
+                acc = psum_s2.tile([P, D_HALF], F32, name="acc", tag="s2")
+                for g in range(HID_PASSES):
+                    nc.tensor.matmul_mx(
+                        out=acc[:],
+                        lhsT=g_codes[:, g, P * a : P * (a + 1)].bitcast(FP8X4),
+                        lhsT_scale=g_scales[:, g, P * a : P * (a + 1)],
+                        rhs=w_codes[:, g, d_cols].bitcast(FP8X4),
+                        rhs_scale=w_scales[:, g, d_cols],
+                        start=(g == 0),
+                        stop=(g == HID_PASSES - 1),
+                    )
+                nc.vector.tensor_tensor(out=resid[:, a, d_cols], in0=acc[:], in1=resid[:, a, d_cols], op=ALU.add)
+            nc.sync.dma_start(out=out_rows[:, a, :], in_=resid[:, a, :])
+
+        for g in range(HID_PASSES):
+            prepare_values(g)
+            prepare_scores(2 * g)
+            prepare_scores(2 * g + 1)
+        for g in range(HID_PASSES):
+            prepare_gate(g)
+            attend(g, 0)
+        for g in range(HID_PASSES):
+            prepare_weights(g)
+        for a in range(TOKEN_BLOCKS):
+            prepare_residual(a)
+        for g in range(HID_PASSES):
+            attend(g, 1)
+            project(g)
+        for a in range(4, TOKEN_BLOCKS):
+            project(a)

@@ -19,10 +19,11 @@ QK = 128
 H = 2048
 D = 1024
 TOKEN_BLOCKS = S // P
+FIRST_BLOCKS = (0, 1, 2, 3)
 KEY_PASSES = S // K_PASS
 HID_PASSES = H // K_PASS
 D_HALF = 512
-RAW_BUFS = 5
+RAW_BUFS = 6
 
 FLOPS = 2 * S * S * QK + 2 * S * S * H + 2 * S * H * D
 
@@ -32,7 +33,7 @@ def tile_gau_pa_kernel(tc, q, k, v, gate, W_out, b_out, x, out):
     q_rows = q.flatten_outer_dims()
     k_rows = k.flatten_outer_dims()
     v_rows = v.flatten_outer_dims()
-    gate_rows = gate.flatten_outer_dims()
+    gate_rows = gate.flatten_outer_dims().rearrange("(p a) h -> p a h", a=TOKEN_BLOCKS)
     x_rows = x.flatten_outer_dims().rearrange("(p a) d -> p a d", a=TOKEN_BLOCKS)
     out_rows = out.flatten_outer_dims().rearrange("(p a) d -> p a d", a=TOKEN_BLOCKS)
 
@@ -44,17 +45,9 @@ def tile_gau_pa_kernel(tc, q, k, v, gate, W_out, b_out, x, out):
         psum_tp = ctx.enter_context(tc.psum_pool(name="psum_tp", bufs=2))
         psum_s1 = ctx.enter_context(tc.psum_pool(name="psum_s1", bufs=3))
         psum_s2 = ctx.enter_context(tc.psum_pool(name="psum_s2", bufs=3))
+        ctx.enter_context(tc.manual_schedule())
 
-        k_sb = keep.tile([P, KEY_PASSES * PACK, QK], BF16, name="k_sb")
-        nc.sync.dma_start(
-            out=k_sb[:].rearrange("p (c t) d -> p c t d", c=KEY_PASSES),
-            in_=k_rows.rearrange("(c p t) d -> p c t d", c=KEY_PASSES, t=PACK),
-        )
-        q_sb = keep.tile([P, TOKEN_BLOCKS, QK], BF16, name="q_sb")
-        nc.sync.dma_start(out=q_sb[:], in_=q_rows.rearrange("(p a) d -> p a d", a=TOKEN_BLOCKS))
-
-        v_raw = []
-        for g in range(HID_PASSES):
+        def load_values(g):
             raw = raw_pool.tile([P, KEY_PASSES * PACK * K_PASS], BF16, name="v_raw%d" % g, tag="raw")
             raw_view = raw[:].rearrange("p (c t h) -> p c t h", c=KEY_PASSES, t=PACK)
             for c in range(KEY_PASSES):
@@ -64,33 +57,43 @@ def tile_gau_pa_kernel(tc, q, k, v, gate, W_out, b_out, x, out):
                         "(p t) h -> p t h", t=PACK
                     ),
                 )
-            v_raw.append(raw)
-        gate_raw = []
-        for g in range(HID_PASSES):
-            raw = raw_pool.tile([P, TOKEN_BLOCKS * K_PASS], BF16, name="gate_raw%d" % g, tag="raw")
+            return raw
+
+        def load_gate(pair):
+            raw = raw_pool.tile([P, 2 * H], BF16, name="gate_raw%d" % pair, tag="raw")
             nc.sync.dma_start(
-                out=raw[:].rearrange("p (a h) -> p a h", a=TOKEN_BLOCKS),
-                in_=gate_rows[:, K_PASS * g : K_PASS * (g + 1)].rearrange("(p a) h -> p a h", a=TOKEN_BLOCKS),
+                out=raw[:].rearrange("p (n h) -> p n h", n=2), in_=gate_rows[:, 2 * pair : 2 * pair + 2, :]
             )
-            gate_raw.append(raw)
-        w_raw = []
-        for g in range(HID_PASSES):
+            return raw
+
+        def load_weights(g):
             raw = raw_pool.tile([P, (D // P) * K_PASS], BF16, name="w_raw%d" % g, tag="raw")
             nc.sync.dma_start(
                 out=raw[:].rearrange("p (a h) -> p a h", a=D // P),
                 in_=W_out[:, K_PASS * g : K_PASS * (g + 1)].rearrange("(a p) h -> p a h", p=P),
             )
-            w_raw.append(raw)
+            return raw
+
+        def load_residual(xh):
+            raw = raw_pool.tile([P, 4 * D], BF16, name="x_raw%d" % xh, tag="raw")
+            nc.sync.dma_start(out=raw[:].rearrange("p (a d) -> p a d", a=4), in_=x_rows[:, 4 * xh : 4 * xh + 4, :])
+            return raw
+
+        k_sb = keep.tile([P, KEY_PASSES * PACK, QK], BF16, name="k_sb")
+        nc.sync.dma_start(
+            out=k_sb[:].rearrange("p (c t) d -> p c t d", c=KEY_PASSES),
+            in_=k_rows.rearrange("(c p t) d -> p c t d", c=KEY_PASSES, t=PACK),
+        )
+        q_sb = keep.tile([P, TOKEN_BLOCKS, QK], BF16, name="q_sb")
+        nc.sync.dma_start(out=q_sb[:], in_=q_rows.rearrange("(p a) d -> p a d", a=TOKEN_BLOCKS))
+        v_raw = [load_values(g) for g in range(3)]
+        gate_raw = [load_gate(pair) for pair in range(2)]
+        v_raw.append(load_values(3))
+        w_raw = [load_weights(g) for g in range(HID_PASSES)]
+        gate_raw.extend([load_gate(pair) for pair in range(2, 4)])
         bias_all = keep.tile([P, D], BF16, name="bias_all")
         nc.sync.dma_start(out=bias_all[:], in_=b_out.partition_broadcast(P))
-        x_raw = []
-        for xh in range(2):
-            raw = raw_pool.tile([P, 4 * D], BF16, name="x_raw%d" % xh, tag="raw")
-            nc.sync.dma_start(
-                out=raw[:].rearrange("p (a d) -> p a d", a=4),
-                in_=x_rows[:, 4 * xh : 4 * xh + 4, :],
-            )
-            x_raw.append(raw)
+        x_raw = [load_residual(xh) for xh in range(2)]
 
         ident_bf = keep.tile([P, P], BF16, name="ident_bf")
         make_identity(nc, ident_bf[:])
@@ -107,10 +110,7 @@ def tile_gau_pa_kernel(tc, q, k, v, gate, W_out, b_out, x, out):
         w_scales = keep.tile([P, HID_PASSES, D], U8, name="w_scales", align_bytes=64)
         g_codes = keep.tile([P, HID_PASSES, S], U32, name="g_codes", align_bytes=64)
         g_scales = keep.tile([P, HID_PASSES, S], U8, name="g_scales", align_bytes=64)
-        gateT = []
-        for g in range(HID_PASSES):
-            gateT_g = keep.tile([P, S * PACK], BF16, name="gateT%d" % g)
-            gateT.append(gateT_g)
+        gateT = [keep.tile([P, S * PACK], BF16, name="gateT%d" % g) for g in range(HID_PASSES)]
         resid = keep.tile([P, TOKEN_BLOCKS, D], F32, name="resid")
 
         for src, dst in ((k_sb, kT), (q_sb, qT)):
@@ -118,12 +118,17 @@ def tile_gau_pa_kernel(tc, q, k, v, gate, W_out, b_out, x, out):
                 tp = psum_tp.tile([P, 4, P], BF16, name="tp_qk", tag="tp")
                 for n in range(4):
                     nc.tensor.transpose(tp[:, n, :], src[:, 4 * half + n, :], ident_bf[:])
-                nc.vector.tensor_copy(out=dst[:, 4 * half : 4 * half + 4, :], in_=tp[:])
+                if half == 0:
+                    nc.vector.tensor_copy(out=dst[:, 0:4, :], in_=tp[:])
+                else:
+                    nc.scalar.copy(out=dst[:, 4:8, :], in_=tp[:])
 
-        def prepare_scores(a):
+        a_grouped = {}
+
+        def scores(a):
             relu_sim = work.tile([P, KEY_PASSES, P, PACK], F32, name="relu_sim", tag="relu_sim")
             for c in range(KEY_PASSES):
-                sim = psum_s1.tile([P, PACK, P], F32, name="sim", tag="s1")
+                sim = psum_s2.tile([P, PACK, P], F32, name="sim", tag="s2")
                 for t in range(PACK):
                     nc.tensor.matmul(
                         out=sim[:, t, :], lhsT=kT[:, PACK * c + t, :], rhs=qT[:, a, :], start=True, stop=True
@@ -138,73 +143,80 @@ def tile_gau_pa_kernel(tc, q, k, v, gate, W_out, b_out, x, out):
             nc.scalar.activation(
                 out=a_grp[:], in_=relu_sim[:].rearrange("p c i t -> p (c i t)"), func=ACT.Square
             )
-            nc.vector.quantize_mx(out=a_codes[:, a, :].bitcast(FP8X4), scales=a_scales[:, a, :], in_=a_grp[:])
+            a_grouped[a] = a_grp
 
-        def prepare_values(g):
-            src = v_raw[g][:].rearrange(
-                "p (c t u m e) -> p c u e m t", c=KEY_PASSES, t=PACK, u=2, e=2
+        def quantise_scores(a):
+            nc.vector.quantize_mx(
+                out=a_codes[:, a, :].bitcast(FP8X4), scales=a_scales[:, a, :], in_=a_grouped[a][:]
             )
-            v_grp = grp_pool.tile([P, KEY_PASSES * K_PASS * PACK], BF16, name="v_grp", tag="grp", align_bytes=64)
-            dst = v_grp[:].rearrange("p (c u e m t) -> p c u e m t", c=KEY_PASSES, u=2, e=2, t=PACK)
+
+        def values(g):
+            src = v_raw[g][:].rearrange("p (c t u m e) -> p c u e m t", c=KEY_PASSES, t=PACK, u=2, e=2)
+            v_grp = grp_pool.tile([P, KEY_PASSES, K_PASS * PACK], BF16, name="v_grp", tag="grp", align_bytes=64)
+            dst = v_grp[:].rearrange("p c (u e m t) -> p c u e m t", u=2, e=2, t=PACK)
             for c in range(KEY_PASSES):
                 nc.vector.tensor_copy(out=dst[:, c, :, :, :, :], in_=src[:, c, :, :, :, :])
-            nc.vector.quantize_mx(out=v_codes[:, g, :].bitcast(FP8X4), scales=v_scales[:, g, :], in_=v_grp[:])
-
-        def transpose_words(raw, dst_words):
-            words = raw[:].bitcast(F32)
-            for pair in range(4):
-                tp = psum_tp.tile([P, 2, 2, P], F32, name="tp_w", tag="tp")
-                for n in range(2):
-                    for u in range(2):
-                        first = 256 * (2 * pair + n) + P * u
-                        nc.tensor.transpose(tp[:, n, u, :], words[:, first : first + P], ident_f32[:])
-                nc.scalar.copy(
-                    out=dst_words[:, 2 * pair : 2 * pair + 2, :, :], in_=tp[:].rearrange("p n u r -> p n r u")
+            for c in range(KEY_PASSES):
+                cols = slice(K_PASS * c, K_PASS * (c + 1))
+                nc.vector.quantize_mx(
+                    out=v_codes[:, g, cols].bitcast(FP8X4), scales=v_scales[:, g, cols], in_=v_grp[:, c, :]
                 )
 
-        def prepare_gate(g):
+        def transpose_words(words, first_words, dst_words):
+            tp = psum_tp.tile([P, 2, 2, P], F32, name="tp_w", tag="tp")
+            for n in range(2):
+                for u in range(2):
+                    first = first_words[n] + P * u
+                    nc.tensor.transpose(tp[:, n, u, :], words[:, first : first + P], ident_f32[:])
+            nc.scalar.copy(out=dst_words, in_=tp[:].rearrange("p n u r -> p n r u"))
+
+        def gate_T(pair, g):
+            dst = gateT[g][:].bitcast(F32).rearrange("p (a r u) -> p a r u", a=TOKEN_BLOCKS, u=2)
             transpose_words(
-                gate_raw[g], gateT[g][:].bitcast(F32).rearrange("p (a r u) -> p a r u", a=TOKEN_BLOCKS, u=2)
+                gate_raw[pair][:].bitcast(F32),
+                [(H // 2) * n + (K_PASS // 2) * g for n in range(2)],
+                dst[:, 2 * pair : 2 * pair + 2, :, :],
             )
 
-        def prepare_weights(g):
+        w_grouped = {}
+
+        def weights_T(g):
             w_grp = grp_pool.tile([P, D * PACK], BF16, name="w_grp", tag="grp", align_bytes=64)
-            transpose_words(w_raw[g], w_grp[:].bitcast(F32).rearrange("p (a r u) -> p a r u", a=D // P, u=2))
-            nc.vector.quantize_mx(out=w_codes[:, g, :].bitcast(FP8X4), scales=w_scales[:, g, :], in_=w_grp[:])
-
-        def attend(g, half):
-            gate_view = gateT[g][:].rearrange("p (a i t) -> p a i t", a=TOKEN_BLOCKS, t=PACK)
-            gated = work.tile([P, 4, P, PACK], BF16, name="gated", tag="gated", align_bytes=64)
-            for n in range(4):
-                a = 4 * half + n
-                av = psum_s1.tile([P, PACK, P], F32, name="av", tag="s1")
-                for t in range(PACK):
-                    for c in range(KEY_PASSES):
-                        v_cols = slice(K_PASS * c + P * t, K_PASS * c + P * (t + 1))
-                        a_cols = slice(P * c, P * (c + 1))
-                        nc.tensor.matmul_mx(
-                            out=av[:, t, :],
-                            lhsT=v_codes[:, g, v_cols].bitcast(FP8X4),
-                            lhsT_scale=v_scales[:, g, v_cols],
-                            rhs=a_codes[:, a, a_cols].bitcast(FP8X4),
-                            rhs_scale=a_scales[:, a, a_cols],
-                            start=(c == 0),
-                            stop=(c == KEY_PASSES - 1),
-                        )
-                nc.vector.tensor_tensor(
-                    out=gated[:, n, :, :],
-                    in0=av[:].rearrange("p t i -> p i t"),
-                    in1=gate_view[:, a, :, :],
-                    op=ALU.mult,
+            dst = w_grp[:].bitcast(F32).rearrange("p (a r u) -> p a r u", a=D // P, u=2)
+            for pair in range(D // P // 2):
+                transpose_words(
+                    w_raw[g][:].bitcast(F32),
+                    [(K_PASS // 2) * (2 * pair + n) for n in range(2)],
+                    dst[:, 2 * pair : 2 * pair + 2, :, :],
                 )
-            cols = slice(4 * P * half, 4 * P * (half + 1))
+            w_grouped[g] = w_grp
+
+        def quantise_weights(g):
             nc.vector.quantize_mx(
-                out=g_codes[:, g, cols].bitcast(FP8X4),
-                scales=g_scales[:, g, cols],
-                in_=gated[:].rearrange("p n i t -> p (n i t)"),
+                out=w_codes[:, g, :].bitcast(FP8X4), scales=w_scales[:, g, :], in_=w_grouped[g][:]
             )
 
-        def prepare_residual(a):
+        def attend(g, a, gated):
+            gate_view = gateT[g][:].rearrange("p (a i t) -> p a i t", a=TOKEN_BLOCKS, t=PACK)
+            av = psum_s1.tile([P, PACK, P], F32, name="av", tag="s1")
+            for t in range(PACK):
+                for c in range(KEY_PASSES):
+                    v_cols = slice(K_PASS * c + P * t, K_PASS * c + P * (t + 1))
+                    a_cols = slice(P * c, P * (c + 1))
+                    nc.tensor.matmul_mx(
+                        out=av[:, t, :],
+                        lhsT=v_codes[:, g, v_cols].bitcast(FP8X4),
+                        lhsT_scale=v_scales[:, g, v_cols],
+                        rhs=a_codes[:, a, a_cols].bitcast(FP8X4),
+                        rhs_scale=a_scales[:, a, a_cols],
+                        start=(c == 0),
+                        stop=(c == KEY_PASSES - 1),
+                    )
+            nc.vector.tensor_tensor(
+                out=gated, in0=av[:].rearrange("p t i -> p i t"), in1=gate_view[:, a, :, :], op=ALU.mult
+            )
+
+        def residual(a):
             x_view = x_raw[a // 4][:].rearrange("p (a d) -> p a d", a=4)
             nc.gpsimd.tensor_tensor(out=resid[:, a, :], in0=x_view[:, a % 4, :], in1=bias_all[:], op=ALU.add)
 
@@ -223,21 +235,57 @@ def tile_gau_pa_kernel(tc, q, k, v, gate, W_out, b_out, x, out):
                         stop=(g == HID_PASSES - 1),
                     )
                 nc.vector.tensor_tensor(out=resid[:, a, d_cols], in0=acc[:], in1=resid[:, a, d_cols], op=ALU.add)
-            nc.sync.dma_start(out=out_rows[:, a, :], in_=resid[:, a, :])
+                nc.sync.dma_start(out=out_rows[:, a, d_cols], in_=resid[:, a, d_cols])
+
+        for g in range(2):
+            scores(2 * g)
+            scores(2 * g + 1)
+            values(g)
+            quantise_scores(2 * g)
+            quantise_scores(2 * g + 1)
+        for pair in range(2):
+            gate_T(pair, 0)
+        values(2)
+        for g in range(HID_PASSES):
+            if g + 1 < HID_PASSES:
+                for pair in range(2):
+                    gate_T(pair, g + 1)
+            gated = work.tile([P, len(FIRST_BLOCKS), P, PACK], BF16, name="gated", tag="gated", align_bytes=64)
+            for a in FIRST_BLOCKS:
+                attend(g, a, gated[:, a, :, :])
+            if g == 0:
+                values(3)
+            else:
+                quantise_weights(g - 1)
+                quantise_scores(3 + g)
+            nc.vector.quantize_mx(
+                out=g_codes[:, g, 0 : 4 * P].bitcast(FP8X4),
+                scales=g_scales[:, g, 0 : 4 * P],
+                in_=gated[:].rearrange("p n i t -> p (n i t)"),
+            )
+            weights_T(g)
+            scores(4 + g)
+        quantise_weights(3)
+        quantise_scores(7)
+        for a in range(TOKEN_BLOCKS):
+            residual(a)
 
         for g in range(HID_PASSES):
-            prepare_values(g)
-            prepare_scores(2 * g)
-            prepare_scores(2 * g + 1)
-        for g in range(HID_PASSES):
-            prepare_gate(g)
-            attend(g, 0)
-        for g in range(HID_PASSES):
-            prepare_weights(g)
-        for a in range(TOKEN_BLOCKS):
-            prepare_residual(a)
-        for g in range(HID_PASSES):
-            attend(g, 1)
+            for pair in range(2, 4):
+                gate_T(pair, g)
             project(g)
+
         for a in range(4, TOKEN_BLOCKS):
-            project(a)
+            gated = work.tile([P, HID_PASSES, P, PACK], BF16, name="gated", tag="gated", align_bytes=64)
+            for g in range(HID_PASSES + 1):
+                if g < HID_PASSES:
+                    attend(g, a, gated[:, g, :, :])
+                if g > 0:
+                    nc.vector.quantize_mx(
+                        out=g_codes[:, g - 1, P * a : P * (a + 1)].bitcast(FP8X4),
+                        scales=g_scales[:, g - 1, P * a : P * (a + 1)],
+                        in_=gated[:, g - 1, :, :].rearrange("p i t -> p (i t)"),
+                    )
+            if a > 4:
+                project(a - 1)
+        project(TOKEN_BLOCKS - 1)

@@ -218,7 +218,7 @@ def tile_gau_pa_kernel(tc, q, k, v, gate, W_out, b_out, x, out):
 
         def residual(a):
             x_view = x_raw[a // 4][:].rearrange("p (a d) -> p a d", a=4)
-            nc.gpsimd.tensor_tensor(out=resid[:, a, :], in0=x_view[:, a % 4, :], in1=bias_all[:], op=ALU.add)
+            nc.vector.tensor_tensor(out=resid[:, a, :], in0=x_view[:, a % 4, :], in1=bias_all[:], op=ALU.add)
 
         def project(a):
             for dh in range(D // D_HALF):
@@ -267,12 +267,11 @@ def tile_gau_pa_kernel(tc, q, k, v, gate, W_out, b_out, x, out):
             scores(4 + g)
         quantise_weights(3)
         quantise_scores(7)
-        for a in range(TOKEN_BLOCKS):
-            residual(a)
 
         for g in range(HID_PASSES):
             for pair in range(2, 4):
                 gate_T(pair, g)
+            residual(g)
             project(g)
 
         for a in range(4, TOKEN_BLOCKS):
@@ -288,4 +287,5 @@ def tile_gau_pa_kernel(tc, q, k, v, gate, W_out, b_out, x, out):
                     )
             if a > 4:
                 project(a - 1)
+            residual(a)
         project(TOKEN_BLOCKS - 1)

@@ -93,7 +93,7 @@ def tile_gau_pa_kernel(tc, q, k, v, gate, W_out, b_out, x, out):
         gate_raw.extend([load_gate(pair) for pair in range(2, 4)])
         bias_all = keep.tile([P, D], BF16, name="bias_all")
         nc.sync.dma_start(out=bias_all[:], in_=b_out.partition_broadcast(P))
-        x_raw = [load_residual(xh) for xh in range(2)]
+        x_raw = [load_residual(0)]
 
         ident_bf = keep.tile([P, P], BF16, name="ident_bf")
         make_identity(nc, ident_bf[:])
@@ -108,8 +108,10 @@ def tile_gau_pa_kernel(tc, q, k, v, gate, W_out, b_out, x, out):
         v_scales = keep.tile([P, HID_PASSES, KEY_PASSES * K_PASS], U8, name="v_scales", align_bytes=64)
         w_codes = keep.tile([P, HID_PASSES, D], U32, name="w_codes", align_bytes=64)
         w_scales = keep.tile([P, HID_PASSES, D], U8, name="w_scales", align_bytes=64)
-        g_codes = keep.tile([P, HID_PASSES, S], U32, name="g_codes", align_bytes=64)
-        g_scales = keep.tile([P, HID_PASSES, S], U8, name="g_scales", align_bytes=64)
+        g_codes_1 = keep.tile([P, HID_PASSES, 4, P], U32, name="g_codes_1", align_bytes=64)
+        g_scales_1 = keep.tile([P, HID_PASSES, 4, P], U8, name="g_scales_1", align_bytes=64)
+        g_codes_2 = keep.tile([P, 4, HID_PASSES, P], U32, name="g_codes_2", align_bytes=64)
+        g_scales_2 = keep.tile([P, 4, HID_PASSES, P], U8, name="g_scales_2", align_bytes=64)
         gateT = [keep.tile([P, S * PACK], BF16, name="gateT%d" % g) for g in range(HID_PASSES)]
         resid = keep.tile([P, TOKEN_BLOCKS, D], F32, name="resid")
 
@@ -150,12 +152,16 @@ def tile_gau_pa_kernel(tc, q, k, v, gate, W_out, b_out, x, out):
                 out=a_codes[:, a, :].bitcast(FP8X4), scales=a_scales[:, a, :], in_=a_grouped[a][:]
             )
 
-        def values(g):
+        def values(g, scalar_helps):
             src = v_raw[g][:].rearrange("p (c t u m e) -> p c u e m t", c=KEY_PASSES, t=PACK, u=2, e=2)
             v_grp = grp_pool.tile([P, KEY_PASSES, K_PASS * PACK], BF16, name="v_grp", tag="grp", align_bytes=64)
             dst = v_grp[:].rearrange("p c (u e m t) -> p c u e m t", u=2, e=2, t=PACK)
-            for c in range(KEY_PASSES):
-                nc.vector.tensor_copy(out=dst[:, c, :, :, :, :], in_=src[:, c, :, :, :, :])
+            nc.vector.tensor_copy(out=dst[:, 0, :, :, :, :], in_=src[:, 0, :, :, :, :])
+            if scalar_helps:
+                for u in range(2):
+                    nc.scalar.copy(out=dst[:, 1, u, :, :, :], in_=src[:, 1, u, :, :, :])
+            else:
+                nc.vector.tensor_copy(out=dst[:, 1, :, :, :, :], in_=src[:, 1, :, :, :, :])
             for c in range(KEY_PASSES):
                 cols = slice(K_PASS * c, K_PASS * (c + 1))
                 nc.vector.quantize_mx(
@@ -216,19 +222,23 @@ def tile_gau_pa_kernel(tc, q, k, v, gate, W_out, b_out, x, out):
                 out=gated, in0=av[:].rearrange("p t i -> p i t"), in1=gate_view[:, a, :, :], op=ALU.mult
             )
 
-        def residual(a):
+        def residual(engine, a):
             x_view = x_raw[a // 4][:].rearrange("p (a d) -> p a d", a=4)
-            nc.vector.tensor_tensor(out=resid[:, a, :], in0=x_view[:, a % 4, :], in1=bias_all[:], op=ALU.add)
+            engine.tensor_tensor(out=resid[:, a, :], in0=x_view[:, a % 4, :], in1=bias_all[:], op=ALU.add)
 
         def project(a):
             for dh in range(D // D_HALF):
                 d_cols = slice(D_HALF * dh, D_HALF * (dh + 1))
                 acc = psum_s2.tile([P, D_HALF], F32, name="acc", tag="s2")
                 for g in range(HID_PASSES):
+                    if a < 4:
+                        codes, scales = g_codes_1[:, g, a, :], g_scales_1[:, g, a, :]
+                    else:
+                        codes, scales = g_codes_2[:, a - 4, g, :], g_scales_2[:, a - 4, g, :]
                     nc.tensor.matmul_mx(
                         out=acc[:],
-                        lhsT=g_codes[:, g, P * a : P * (a + 1)].bitcast(FP8X4),
-                        lhsT_scale=g_scales[:, g, P * a : P * (a + 1)],
+                        lhsT=codes.bitcast(FP8X4),
+                        lhsT_scale=scales,
                         rhs=w_codes[:, g, d_cols].bitcast(FP8X4),
                         rhs_scale=w_scales[:, g, d_cols],
                         start=(g == 0),
@@ -240,12 +250,12 @@ def tile_gau_pa_kernel(tc, q, k, v, gate, W_out, b_out, x, out):
         for g in range(2):
             scores(2 * g)
             scores(2 * g + 1)
-            values(g)
+            values(g, False)
             quantise_scores(2 * g)
             quantise_scores(2 * g + 1)
         for pair in range(2):
             gate_T(pair, 0)
-        values(2)
+        values(2, False)
         for g in range(HID_PASSES):
             if g + 1 < HID_PASSES:
                 for pair in range(2):
@@ -254,13 +264,13 @@ def tile_gau_pa_kernel(tc, q, k, v, gate, W_out, b_out, x, out):
             for a in FIRST_BLOCKS:
                 attend(g, a, gated[:, a, :, :])
             if g == 0:
-                values(3)
+                values(3, True)
             else:
                 quantise_weights(g - 1)
                 quantise_scores(3 + g)
             nc.vector.quantize_mx(
-                out=g_codes[:, g, 0 : 4 * P].bitcast(FP8X4),
-                scales=g_scales[:, g, 0 : 4 * P],
+                out=g_codes_1[:, g, :, :].rearrange("p n i -> p (n i)").bitcast(FP8X4),
+                scales=g_scales_1[:, g, :, :].rearrange("p n i -> p (n i)"),
                 in_=gated[:].rearrange("p n i t -> p (n i t)"),
             )
             weights_T(g)
@@ -271,21 +281,22 @@ def tile_gau_pa_kernel(tc, q, k, v, gate, W_out, b_out, x, out):
         for g in range(HID_PASSES):
             for pair in range(2, 4):
                 gate_T(pair, g)
-            residual(g)
+            residual(nc.vector, g)
             project(g)
+            if g == 0:
+                x_raw.append(load_residual(1))
+        for a in range(4, TOKEN_BLOCKS):
+            residual(nc.gpsimd, a)
 
         for a in range(4, TOKEN_BLOCKS):
             gated = work.tile([P, HID_PASSES, P, PACK], BF16, name="gated", tag="gated", align_bytes=64)
-            for g in range(HID_PASSES + 1):
-                if g < HID_PASSES:
-                    attend(g, a, gated[:, g, :, :])
-                if g > 0:
-                    nc.vector.quantize_mx(
-                        out=g_codes[:, g - 1, P * a : P * (a + 1)].bitcast(FP8X4),
-                        scales=g_scales[:, g - 1, P * a : P * (a + 1)],
-                        in_=gated[:, g - 1, :, :].rearrange("p i t -> p (i t)"),
-                    )
+            for g in range(HID_PASSES):
+                attend(g, a, gated[:, g, :, :])
+            nc.vector.quantize_mx(
+                out=g_codes_2[:, a - 4, :, :].rearrange("p g i -> p (g i)").bitcast(FP8X4),
+                scales=g_scales_2[:, a - 4, :, :].rearrange("p g i -> p (g i)"),
+                in_=gated[:].rearrange("p g i t -> p (g i t)"),
+            )
             if a > 4:
                 project(a - 1)
-            residual(a)
         project(TOKEN_BLOCKS - 1)

@@ -153,15 +153,13 @@ def tile_gau_pa_kernel(tc, q, k, v, gate, W_out, b_out, x, out):
             )
 
         def values(g, scalar_helps):
-            src = v_raw[g][:].rearrange("p (c t u m e) -> p c u e m t", c=KEY_PASSES, t=PACK, u=2, e=2)
+            src = v_raw[g][:].rearrange("p (c t u n j e) -> p c u n t j e", c=KEY_PASSES, t=PACK, u=2, j=2, e=2)
             v_grp = grp_pool.tile([P, KEY_PASSES, K_PASS * PACK], BF16, name="v_grp", tag="grp", align_bytes=64)
-            dst = v_grp[:].rearrange("p c (u e m t) -> p c u e m t", u=2, e=2, t=PACK)
-            nc.vector.tensor_copy(out=dst[:, 0, :, :, :, :], in_=src[:, 0, :, :, :, :])
-            if scalar_helps:
+            dst = v_grp[:].rearrange("p c (u e n j t) -> p c u n t j e", u=2, e=2, j=2, t=PACK)
+            for c in range(KEY_PASSES):
                 for u in range(2):
-                    nc.scalar.copy(out=dst[:, 1, u, :, :, :], in_=src[:, 1, u, :, :, :])
-            else:
-                nc.vector.tensor_copy(out=dst[:, 1, :, :, :, :], in_=src[:, 1, :, :, :, :])
+                    copy = nc.scalar.copy if scalar_helps and c == 1 else nc.vector.tensor_copy
+                    copy(out=dst[:, c, u, :, :, :, :], in_=src[:, c, u, :, :, :, :])
             for c in range(KEY_PASSES):
                 cols = slice(K_PASS * c, K_PASS * (c + 1))
                 nc.vector.quantize_mx(

@@ -18,14 +18,36 @@ S = 1024
 QK = 128
 H = 2048
 D = 1024
-TOKEN_BLOCKS = S // P
-FIRST_BLOCKS = (0, 1, 2, 3)
+BLOCKS = S // P
 KEY_PASSES = S // K_PASS
 HID_PASSES = H // K_PASS
 D_HALF = 512
-RAW_BUFS = 6
 
 FLOPS = 2 * S * S * QK + 2 * S * S * H + 2 * S * H * D
+
+LOADS = """ld.k.0 ld.q.0 ld.v.0 ld.v.1 ld.v.2 ld.g.0 ld.g.1 ld.v.3 ld.g.2 ld.g.3 ld.W.0 ld.W.1 ld.W.2 ld.W.3 ld.g.4
+ld.g.5 ld.b.0 ld.g.6 ld.g.7"""
+TENSOR = """T.k.0 T.k.1 T.q.0 T.q.1 sc.0.0 sc.0.1 sc.1.0 sc.1.1 sc.2.0 sc.2.1 av.0.0 sc.3.0 sc.3.1 av.1.0 sc.4.0 sc.4.1
+av.2.0 av.0.1 av.1.1 sc.5.0 sc.5.1 av.2.1 vt.0.0 vt.1.0 wt.0.0 av.0.2 av.1.2 av.2.2 vt.2.0 wt.0.1 wt.0.2
+wt.0.3 av.0.3 av.1.3 av.2.3 wt.1.0 wt.1.1 av.3.0 av.3.1 vt.0.1 vt.1.1 wt.1.2 wt.1.3 av.3.2 av.3.3 vt.2.1
+wt.2.0 wt.2.1 sc.6.0 sc.6.1 av.4.0 av.4.1 vt.3.0 vt.3.1 wt.2.2 wt.2.3 wt.3.0 av.4.2 av.4.3 av.5.0 wt.3.1
+wt.3.2 wt.3.3 vt.4.0 vt.4.1 sc.7.0 sc.7.1 av.5.1 av.5.2 av.5.3 pj.0.0 pj.0.1 av.6.0 av.6.1 vt.5.0 vt.5.1
+pj.1.0 pj.1.1 av.6.2 av.6.3 pj.2.0 pj.2.1 vt.6.0 vt.6.1 av.7.0 av.7.1 pj.3.0 pj.3.1 av.7.2 av.7.3 pj.4.0
+pj.4.1 vt.7.0 vt.7.1 pj.5.0 pj.5.1 pj.6.0 pj.6.1 pj.7.0 pj.7.1"""
+SCALAR = """C.k.1 C.q.1 re.0.0 re.0.1 re.1.0 sq.0 re.1.1 re.2.0 sq.1 re.2.1 re.3.0 sq.2 re.3.1 re.4.0 sq.3 re.4.1 re.5.0
+sq.4 re.5.1 sq.5 ve.0.0 ve.1.0 we.0.0 ve.2.0 we.0.1 we.0.2 we.0.3 we.1.0 we.1.1 ve.0.1 ve.1.1 we.1.2 we.1.3
+ve.2.1 we.2.0 we.2.1 ld.x.0 re.6.0 re.6.1 ve.3.0 sq.6 ve.3.1 we.2.2 we.2.3 we.3.0 we.3.1 we.3.2 we.3.3 ve.4.0
+ve.4.1 ld.x.1 re.7.0 re.7.1 sq.7 ve.5.0 ve.5.1 ve.6.0 ve.6.1 ve.7.0 ve.7.1"""
+VECTOR = """C.k.0 C.q.0 vc.0.0.0 vc.0.0.1 vc.0.1.0 vc.0.1.1 qv.0.0 qv.0.1 vc.1.0.0 qA.0 vc.1.0.1 vc.1.1.0 vc.1.1.1 qA.1
+qv.1.0 qv.1.1 vc.2.0.0 vc.2.0.1 ga.0.0 qA.2 vc.2.1.0 vc.2.1.1 ga.1.0 qv.2.0 ga.0.1 qv.2.1 ga.2.0 vc.3.0.0
+vc.3.0.1 ga.1.1 vc.3.1.0 vc.3.1.1 ga.2.1 qA.3 qv.3.0 qV.0.0 qv.3.1 qV.1.0 ga.0.2 qA.4 ga.1.2 qV.2.0 ga.2.2
+qW.0.0 ga.0.3 ga.1.3 qW.0.1 ga.2.3 ga.3.0 qA.5 ga.3.1 qV.0.1 qW.1.0 qV.1.1 ga.3.2 qW.1.1 qV.2.1 ga.3.3 ga.4.0
+ga.4.1 qW.2.0 qV.3.0 qV.3.1 ga.4.2 qW.2.1 ga.4.3 qA.6 ga.5.0 qW.3.0 qV.4.0 qV.4.1 ga.5.1 qW.3.1 ga.5.2 ga.5.3
+fi.0.0 fi.0.1 qA.7 ga.6.0 ga.6.1 qV.5.0 qV.5.1 fi.1.0 fi.1.1 ga.6.2 ga.6.3 fi.2.0 fi.2.1 qV.6.0 qV.6.1 ga.7.0
+ga.7.1 fi.3.0 fi.3.1 ga.7.2 ga.7.3 fi.4.0 fi.4.1 qV.7.0 qV.7.1 fi.5.0 fi.5.1 fi.6.0 fi.6.1 fi.7.0 fi.7.1"""
+GPSIMD = "rs.0 rs.1 rs.2 rs.3 rs.4 rs.5 rs.6 rs.7"
+
+RING_BUFS = {"raw":5,"gate":6,"relu":3,"a_grp":4,"grp":2,"gated":8,"v_t":4,"resid":4,"ps":4,"pv":4}
 
 
 def tile_gau_pa_kernel(tc, q, k, v, gate, W_out, b_out, x, out):
@@ -33,268 +55,318 @@ def tile_gau_pa_kernel(tc, q, k, v, gate, W_out, b_out, x, out):
     q_rows = q.flatten_outer_dims()
     k_rows = k.flatten_outer_dims()
     v_rows = v.flatten_outer_dims()
-    gate_rows = gate.flatten_outer_dims().rearrange("(p a) h -> p a h", a=TOKEN_BLOCKS)
-    x_rows = x.flatten_outer_dims().rearrange("(p a) d -> p a d", a=TOKEN_BLOCKS)
-    out_rows = out.flatten_outer_dims().rearrange("(p a) d -> p a d", a=TOKEN_BLOCKS)
+    gate_rows = gate.flatten_outer_dims().rearrange("(p a) h -> p a h", a=BLOCKS)
+    x_rows = x.flatten_outer_dims().rearrange("(p a) d -> p a d", a=BLOCKS)
+    out_rows = out.flatten_outer_dims().rearrange("(p a) d -> p a d", a=BLOCKS)
 
     with ExitStack() as ctx:
         keep = ctx.enter_context(tc.tile_pool(name="keep", bufs=1))
-        raw_pool = ctx.enter_context(tc.tile_pool(name="raw", bufs=RAW_BUFS))
-        grp_pool = ctx.enter_context(tc.tile_pool(name="grp", bufs=2))
-        work = ctx.enter_context(tc.tile_pool(name="work", bufs=2))
-        psum_tp = ctx.enter_context(tc.psum_pool(name="psum_tp", bufs=2))
-        psum_s1 = ctx.enter_context(tc.psum_pool(name="psum_s1", bufs=3))
-        psum_s2 = ctx.enter_context(tc.psum_pool(name="psum_s2", bufs=3))
+        sbuf = ctx.enter_context(tc.tile_pool(name="sbuf", bufs=1))
+        psum_s = ctx.enter_context(tc.psum_pool(name="psum_s", bufs=RING_BUFS["ps"]))
+        psum_v = ctx.enter_context(tc.psum_pool(name="psum_v", bufs=RING_BUFS["pv"]))
         ctx.enter_context(tc.manual_schedule())
 
-        def load_values(g):
-            raw = raw_pool.tile([P, KEY_PASSES * PACK * K_PASS], BF16, name="v_raw%d" % g, tag="raw")
-            raw_view = raw[:].rearrange("p (c t h) -> p c t h", c=KEY_PASSES, t=PACK)
-            for c in range(KEY_PASSES):
-                nc.sync.dma_start(
-                    out=raw_view[:, c, :, :],
-                    in_=v_rows[K_PASS * c : K_PASS * (c + 1), K_PASS * g : K_PASS * (g + 1)].rearrange(
-                        "(p t) h -> p t h", t=PACK
-                    ),
-                )
-            return raw
-
-        def load_gate(pair):
-            raw = raw_pool.tile([P, 2 * H], BF16, name="gate_raw%d" % pair, tag="raw")
-            nc.sync.dma_start(
-                out=raw[:].rearrange("p (n h) -> p n h", n=2), in_=gate_rows[:, 2 * pair : 2 * pair + 2, :]
-            )
-            return raw
-
-        def load_weights(g):
-            raw = raw_pool.tile([P, (D // P) * K_PASS], BF16, name="w_raw%d" % g, tag="raw")
-            nc.sync.dma_start(
-                out=raw[:].rearrange("p (a h) -> p a h", a=D // P),
-                in_=W_out[:, K_PASS * g : K_PASS * (g + 1)].rearrange("(a p) h -> p a h", p=P),
-            )
-            return raw
-
-        def load_residual(xh):
-            raw = raw_pool.tile([P, 4 * D], BF16, name="x_raw%d" % xh, tag="raw")
-            nc.sync.dma_start(out=raw[:].rearrange("p (a d) -> p a d", a=4), in_=x_rows[:, 4 * xh : 4 * xh + 4, :])
-            return raw
-
         k_sb = keep.tile([P, KEY_PASSES * PACK, QK], BF16, name="k_sb")
-        nc.sync.dma_start(
-            out=k_sb[:].rearrange("p (c t) d -> p c t d", c=KEY_PASSES),
-            in_=k_rows.rearrange("(c p t) d -> p c t d", c=KEY_PASSES, t=PACK),
-        )
-        q_sb = keep.tile([P, TOKEN_BLOCKS, QK], BF16, name="q_sb")
-        nc.sync.dma_start(out=q_sb[:], in_=q_rows.rearrange("(p a) d -> p a d", a=TOKEN_BLOCKS))
-        v_raw = [load_values(g) for g in range(3)]
-        gate_raw = [load_gate(pair) for pair in range(2)]
-        v_raw.append(load_values(3))
-        w_raw = [load_weights(g) for g in range(HID_PASSES)]
-        gate_raw.extend([load_gate(pair) for pair in range(2, 4)])
+        q_sb = keep.tile([P, BLOCKS, QK], BF16, name="q_sb")
         bias_all = keep.tile([P, D], BF16, name="bias_all")
-        nc.sync.dma_start(out=bias_all[:], in_=b_out.partition_broadcast(P))
-        x_raw = [load_residual(0)]
-
         ident_bf = keep.tile([P, P], BF16, name="ident_bf")
-        make_identity(nc, ident_bf[:])
         ident_f32 = keep.tile([P, P], F32, name="ident_f32")
-        make_identity(nc, ident_f32[:])
-
         kT = keep.tile([P, KEY_PASSES * PACK, P], BF16, name="kT")
-        qT = keep.tile([P, TOKEN_BLOCKS, P], BF16, name="qT")
-        a_codes = keep.tile([P, TOKEN_BLOCKS, KEY_PASSES * P], U32, name="a_codes", align_bytes=64)
-        a_scales = keep.tile([P, TOKEN_BLOCKS, KEY_PASSES * P], U8, name="a_scales", align_bytes=64)
+        qT = keep.tile([P, BLOCKS, P], BF16, name="qT")
+        a_codes = keep.tile([P, BLOCKS, KEY_PASSES * P], U32, name="a_codes", align_bytes=64)
+        a_scales = keep.tile([P, BLOCKS, KEY_PASSES * P], U8, name="a_scales", align_bytes=64)
         v_codes = keep.tile([P, HID_PASSES, KEY_PASSES * K_PASS], U32, name="v_codes", align_bytes=64)
         v_scales = keep.tile([P, HID_PASSES, KEY_PASSES * K_PASS], U8, name="v_scales", align_bytes=64)
         w_codes = keep.tile([P, HID_PASSES, D], U32, name="w_codes", align_bytes=64)
         w_scales = keep.tile([P, HID_PASSES, D], U8, name="w_scales", align_bytes=64)
-        g_codes_1 = keep.tile([P, HID_PASSES, 4, P], U32, name="g_codes_1", align_bytes=64)
-        g_scales_1 = keep.tile([P, HID_PASSES, 4, P], U8, name="g_scales_1", align_bytes=64)
-        g_codes_2 = keep.tile([P, 4, HID_PASSES, P], U32, name="g_codes_2", align_bytes=64)
-        g_scales_2 = keep.tile([P, 4, HID_PASSES, P], U8, name="g_scales_2", align_bytes=64)
-        gateT = [keep.tile([P, S * PACK], BF16, name="gateT%d" % g) for g in range(HID_PASSES)]
-        resid = keep.tile([P, TOKEN_BLOCKS, D], F32, name="resid")
+        g_codes = keep.tile([P, BLOCKS, HID_PASSES * P], U32, name="g_codes", align_bytes=64)
+        g_scales = keep.tile([P, BLOCKS, HID_PASSES * P], U8, name="g_scales", align_bytes=64)
+        make_identity(nc, ident_bf[:])
+        make_identity(nc, ident_f32[:])
 
-        for src, dst in ((k_sb, kT), (q_sb, qT)):
-            for half in range(2):
-                tp = psum_tp.tile([P, 4, P], BF16, name="tp_qk", tag="tp")
-                for n in range(4):
-                    nc.tensor.transpose(tp[:, n, :], src[:, 4 * half + n, :], ident_bf[:])
-                if half == 0:
-                    nc.vector.tensor_copy(out=dst[:, 0:4, :], in_=tp[:])
-                else:
-                    nc.scalar.copy(out=dst[:, 4:8, :], in_=tp[:])
+        tiles = {}
 
-        a_grouped = {}
+        def ring_tile(tag, key, shape, dtype):
+            tiles[key] = sbuf.tile(shape, dtype, name=tag, tag=tag, bufs=RING_BUFS[tag], align_bytes=64)
+            return tiles[key]
 
-        def scores(a):
-            relu_sim = work.tile([P, KEY_PASSES, P, PACK], F32, name="relu_sim", tag="relu_sim")
-            for c in range(KEY_PASSES):
-                sim = psum_s2.tile([P, PACK, P], F32, name="sim", tag="s2")
-                for t in range(PACK):
-                    nc.tensor.matmul(
-                        out=sim[:, t, :], lhsT=kT[:, PACK * c + t, :], rhs=qT[:, a, :], start=True, stop=True
+        def psum_tile(pool, key, shape, dtype):
+            tiles[key] = pool.tile(shape, dtype, name="bank", tag="bank")
+            return tiles[key]
+
+        def load(what, i, queue):
+            if what == "k":
+                nc.sync.dma_start(
+                    out=k_sb[:].rearrange("p (c t) d -> p c t d", c=KEY_PASSES),
+                    in_=k_rows.rearrange("(c p t) d -> p c t d", c=KEY_PASSES, t=PACK),
+                )
+            elif what == "q":
+                nc.sync.dma_start(out=q_sb[:], in_=q_rows.rearrange("(p a) d -> p a d", a=BLOCKS))
+            elif what == "b":
+                nc.sync.dma_start(out=bias_all[:], in_=b_out.partition_broadcast(P))
+            elif what == "v":
+                raw = ring_tile("raw", ("v", i), [P, KEY_PASSES * PACK * K_PASS], BF16)
+                view = raw[:].rearrange("p (c t h) -> p c t h", c=KEY_PASSES, t=PACK)
+                for c in range(KEY_PASSES):
+                    nc.sync.dma_start(
+                        out=view[:, c, :, :],
+                        in_=v_rows[K_PASS * c : K_PASS * (c + 1), K_PASS * i : K_PASS * (i + 1)].rearrange(
+                            "(p t) h -> p t h", t=PACK
+                        ),
                     )
-                nc.scalar.activation(
-                    out=relu_sim[:, c, :, :],
-                    in_=sim[:].rearrange("p t i -> p i t"),
-                    func=ACT.Relu,
-                    scale=1.0 / S,
+            elif what == "g":
+                raw = ring_tile("gate", ("g", i), [P, H], BF16)
+                nc.sync.dma_start(out=raw[:], in_=gate_rows[:, i, :])
+            elif what == "W":
+                raw = ring_tile("raw", ("W", i), [P, (D // P) * K_PASS], BF16)
+                nc.sync.dma_start(
+                    out=raw[:].rearrange("p (a h) -> p a h", a=D // P),
+                    in_=W_out[:, K_PASS * i : K_PASS * (i + 1)].rearrange("(a p) h -> p a h", p=P),
                 )
-            a_grp = work.tile([P, KEY_PASSES * P * PACK], BF16, name="a_grp", tag="a_grp", align_bytes=64)
+            else:
+                raw = ring_tile("raw", ("x", i), [P, 4 * D], BF16)
+                queue.dma_start(
+                    out=raw[:].rearrange("p (a d) -> p a d", a=4), in_=x_rows[:, 4 * i : 4 * i + 4, :]
+                )
+
+        def turn_qk(what, half):
+            src = k_sb if what == "k" else q_sb
+            bank = psum_tile(psum_s, ("T" + what, half), [P, 4, P], BF16)
+            for n in range(4):
+                nc.tensor.transpose(bank[:, n, :], src[:, 4 * half + n, :], ident_bf[:])
+
+        def keep_qk(what, half, copy):
+            dst = kT if what == "k" else qT
+            copy(out=dst[:, 4 * half : 4 * half + 4, :], in_=tiles[("T" + what, half)][:])
+
+        def sim(a, c):
+            bank = psum_tile(psum_s, ("sc", a, c), [P, PACK, P], F32)
+            for t in range(PACK):
+                nc.tensor.matmul(
+                    out=bank[:, t, :], lhsT=kT[:, PACK * c + t, :], rhs=qT[:, a, :], start=True, stop=True
+                )
+
+        def relu(a, c):
+            if c == 0:
+                ring_tile("relu", ("re", a), [P, KEY_PASSES, P, PACK], F32)
             nc.scalar.activation(
-                out=a_grp[:], in_=relu_sim[:].rearrange("p c i t -> p (c i t)"), func=ACT.Square
+                out=tiles[("re", a)][:, c, :, :],
+                in_=tiles[("sc", a, c)][:].rearrange("p t i -> p i t"),
+                func=ACT.Relu,
+                scale=1.0 / S,
             )
-            a_grouped[a] = a_grp
 
-        def quantise_scores(a):
+        def square(a):
+            grp = ring_tile("a_grp", ("sq", a), [P, KEY_PASSES * P * PACK], BF16)
+            nc.scalar.activation(
+                out=grp[:], in_=tiles[("re", a)][:].rearrange("p c i t -> p (c i t)"), func=ACT.Square
+            )
+
+        def quantise_a(a):
             nc.vector.quantize_mx(
-                out=a_codes[:, a, :].bitcast(FP8X4), scales=a_scales[:, a, :], in_=a_grouped[a][:]
+                out=a_codes[:, a, :].bitcast(FP8X4), scales=a_scales[:, a, :], in_=tiles[("sq", a)][:]
             )
 
-        def values(g, scalar_helps):
-            src = v_raw[g][:].rearrange("p (c t u n j e) -> p c u n t j e", c=KEY_PASSES, t=PACK, u=2, j=2, e=2)
-            v_grp = grp_pool.tile([P, KEY_PASSES, K_PASS * PACK], BF16, name="v_grp", tag="grp", align_bytes=64)
-            dst = v_grp[:].rearrange("p c (u e n j t) -> p c u n t j e", u=2, e=2, j=2, t=PACK)
+        def group_v(g, c, half, copy):
+            if ("vg", g) not in tiles:
+                ring_tile("grp", ("vg", g), [P, KEY_PASSES, K_PASS * PACK], BF16)
+            src = tiles[("v", g)][:].rearrange("p (c t n i) -> p c n t i", c=KEY_PASSES, t=PACK, i=4)
+            dst = tiles[("vg", g)][:].rearrange("p c (n i t) -> p c n t i", i=4, t=PACK)
+            rows = slice(64 * half, 64 * half + 64)
+            copy(out=dst[:, c, rows, :, :], in_=src[:, c, rows, :, :])
+
+        def quantise_v(g, c):
+            cols = slice(K_PASS * c, K_PASS * (c + 1))
+            nc.vector.quantize_mx(
+                out=v_codes[:, g, cols].bitcast(FP8X4), scales=v_scales[:, g, cols], in_=tiles[("vg", g)][:, c, :]
+            )
+
+        def attend(a, g):
+            bank = psum_tile(psum_v, ("av", a, g), [P, K_PASS], F32)
             for c in range(KEY_PASSES):
-                for u in range(2):
-                    copy = nc.scalar.copy if scalar_helps and c == 1 else nc.vector.tensor_copy
-                    copy(out=dst[:, c, u, :, :, :, :], in_=src[:, c, u, :, :, :, :])
-            for c in range(KEY_PASSES):
-                cols = slice(K_PASS * c, K_PASS * (c + 1))
-                nc.vector.quantize_mx(
-                    out=v_codes[:, g, cols].bitcast(FP8X4), scales=v_scales[:, g, cols], in_=v_grp[:, c, :]
+                a_cols = slice(P * c, P * (c + 1))
+                v_cols = slice(K_PASS * c, K_PASS * (c + 1))
+                nc.tensor.matmul_mx(
+                    out=bank[:],
+                    lhsT=a_codes[:, a, a_cols].bitcast(FP8X4),
+                    lhsT_scale=a_scales[:, a, a_cols],
+                    rhs=v_codes[:, g, v_cols].bitcast(FP8X4),
+                    rhs_scale=v_scales[:, g, v_cols],
+                    start=(c == 0),
+                    stop=(c == KEY_PASSES - 1),
                 )
 
-        def transpose_words(words, first_words, dst_words):
-            tp = psum_tp.tile([P, 2, 2, P], F32, name="tp_w", tag="tp")
+        def apply_gate(a, g):
+            if g % 2 == 0:
+                ring_tile("gated", ("ga", a, g // 2), [P, 2 * K_PASS], BF16)
+            cols = slice(K_PASS * (g % 2), K_PASS * (g % 2 + 1))
+            nc.vector.tensor_tensor(
+                out=tiles[("ga", a, g // 2)][:, cols],
+                in0=tiles[("av", a, g)][:],
+                in1=tiles[("g", a)][:, K_PASS * g : K_PASS * (g + 1)],
+                op=ALU.mult,
+            )
+
+        def turn_words(key, words):
+            bank = psum_tile(psum_s, key, [P, 2, 2, P], F32)
             for n in range(2):
                 for u in range(2):
-                    first = first_words[n] + P * u
-                    nc.tensor.transpose(tp[:, n, u, :], words[:, first : first + P], ident_f32[:])
-            nc.scalar.copy(out=dst_words, in_=tp[:].rearrange("p n u r -> p n r u"))
+                    first = 2 * P * n + P * u
+                    nc.tensor.transpose(bank[:, n, u, :], words[:, first : first + P], ident_f32[:])
 
-        def gate_T(pair, g):
-            dst = gateT[g][:].bitcast(F32).rearrange("p (a r u) -> p a r u", a=TOKEN_BLOCKS, u=2)
-            transpose_words(
-                gate_raw[pair][:].bitcast(F32),
-                [(H // 2) * n + (K_PASS // 2) * g for n in range(2)],
-                dst[:, 2 * pair : 2 * pair + 2, :, :],
+        def turn_v(a, h):
+            turn_words(("vt", a, h), tiles[("ga", a, h)][:].bitcast(F32))
+
+        def keep_v(a, h):
+            grp = ring_tile("v_t", ("ve", a, h), [P, 2 * K_PASS], BF16)
+            nc.scalar.copy(
+                out=grp[:].bitcast(F32).rearrange("p (n r u) -> p n r u", n=2, u=2),
+                in_=tiles[("vt", a, h)][:].rearrange("p n u r -> p n r u"),
             )
 
-        w_grouped = {}
+        def quantise_g(a, h):
+            cols = slice(2 * P * h, 2 * P * (h + 1))
+            nc.vector.quantize_mx(
+                out=g_codes[:, a, cols].bitcast(FP8X4), scales=g_scales[:, a, cols], in_=tiles[("ve", a, h)][:]
+            )
 
-        def weights_T(g):
-            w_grp = grp_pool.tile([P, D * PACK], BF16, name="w_grp", tag="grp", align_bytes=64)
-            dst = w_grp[:].bitcast(F32).rearrange("p (a r u) -> p a r u", a=D // P, u=2)
-            for pair in range(D // P // 2):
-                transpose_words(
-                    w_raw[g][:].bitcast(F32),
-                    [(K_PASS // 2) * (2 * pair + n) for n in range(2)],
-                    dst[:, 2 * pair : 2 * pair + 2, :, :],
+        def turn_w(g, pair):
+            words = tiles[("W", g)][:].bitcast(F32)
+            turn_words(("wt", g, pair), words[:, 4 * P * pair : 4 * P * (pair + 1)])
+
+        def keep_w(g, pair):
+            if ("wg", g) not in tiles:
+                ring_tile("grp", ("wg", g), [P, KEY_PASSES, K_PASS * PACK], BF16)
+            dst = tiles[("wg", g)][:].rearrange("p c w -> p (c w)").bitcast(F32)
+            dst = dst.rearrange("p (n r u) -> p n r u", n=D // P, u=2)
+            nc.scalar.copy(
+                out=dst[:, 2 * pair : 2 * pair + 2, :, :],
+                in_=tiles[("wt", g, pair)][:].rearrange("p n u r -> p n r u"),
+            )
+
+        def quantise_w(g, half):
+            cols = slice(D_HALF * half, D_HALF * (half + 1))
+            nc.vector.quantize_mx(
+                out=w_codes[:, g, cols].bitcast(FP8X4),
+                scales=w_scales[:, g, cols],
+                in_=tiles[("wg", g)][:, half, :],
+            )
+
+        def residual(a):
+            res = ring_tile("resid", ("rs", a), [P, D], F32)
+            for n in range(4):
+                cols = slice(256 * n, 256 * (n + 1))
+                x_view = tiles[("x", a // 4)][:].rearrange("p (a d) -> p a d", a=4)
+                nc.gpsimd.tensor_tensor(
+                    out=res[:, cols], in0=x_view[:, a % 4, cols], in1=bias_all[:, cols], op=ALU.add
                 )
-            w_grouped[g] = w_grp
 
-        def quantise_weights(g):
-            nc.vector.quantize_mx(
-                out=w_codes[:, g, :].bitcast(FP8X4), scales=w_scales[:, g, :], in_=w_grouped[g][:]
-            )
-
-        def attend(g, a, gated):
-            gate_view = gateT[g][:].rearrange("p (a i t) -> p a i t", a=TOKEN_BLOCKS, t=PACK)
-            av = psum_s1.tile([P, PACK, P], F32, name="av", tag="s1")
-            for t in range(PACK):
-                for c in range(KEY_PASSES):
-                    v_cols = slice(K_PASS * c + P * t, K_PASS * c + P * (t + 1))
-                    a_cols = slice(P * c, P * (c + 1))
-                    nc.tensor.matmul_mx(
-                        out=av[:, t, :],
-                        lhsT=v_codes[:, g, v_cols].bitcast(FP8X4),
-                        lhsT_scale=v_scales[:, g, v_cols],
-                        rhs=a_codes[:, a, a_cols].bitcast(FP8X4),
-                        rhs_scale=a_scales[:, a, a_cols],
-                        start=(c == 0),
-                        stop=(c == KEY_PASSES - 1),
-                    )
-            nc.vector.tensor_tensor(
-                out=gated, in0=av[:].rearrange("p t i -> p i t"), in1=gate_view[:, a, :, :], op=ALU.mult
-            )
-
-        def residual(engine, a):
-            x_view = x_raw[a // 4][:].rearrange("p (a d) -> p a d", a=4)
-            engine.tensor_tensor(out=resid[:, a, :], in0=x_view[:, a % 4, :], in1=bias_all[:], op=ALU.add)
-
-        def project(a):
-            for dh in range(D // D_HALF):
-                d_cols = slice(D_HALF * dh, D_HALF * (dh + 1))
-                acc = psum_s2.tile([P, D_HALF], F32, name="acc", tag="s2")
-                for g in range(HID_PASSES):
-                    if a < 4:
-                        codes, scales = g_codes_1[:, g, a, :], g_scales_1[:, g, a, :]
-                    else:
-                        codes, scales = g_codes_2[:, a - 4, g, :], g_scales_2[:, a - 4, g, :]
-                    nc.tensor.matmul_mx(
-                        out=acc[:],
-                        lhsT=codes.bitcast(FP8X4),
-                        lhsT_scale=scales,
-                        rhs=w_codes[:, g, d_cols].bitcast(FP8X4),
-                        rhs_scale=w_scales[:, g, d_cols],
-                        start=(g == 0),
-                        stop=(g == HID_PASSES - 1),
-                    )
-                nc.vector.tensor_tensor(out=resid[:, a, d_cols], in0=acc[:], in1=resid[:, a, d_cols], op=ALU.add)
-                nc.sync.dma_start(out=out_rows[:, a, d_cols], in_=resid[:, a, d_cols])
-
-        for g in range(2):
-            scores(2 * g)
-            scores(2 * g + 1)
-            values(g, False)
-            quantise_scores(2 * g)
-            quantise_scores(2 * g + 1)
-        for pair in range(2):
-            gate_T(pair, 0)
-        values(2, False)
-        for g in range(HID_PASSES):
-            if g + 1 < HID_PASSES:
-                for pair in range(2):
-                    gate_T(pair, g + 1)
-            gated = work.tile([P, len(FIRST_BLOCKS), P, PACK], BF16, name="gated", tag="gated", align_bytes=64)
-            for a in FIRST_BLOCKS:
-                attend(g, a, gated[:, a, :, :])
-            if g == 0:
-                values(3, True)
-            else:
-                quantise_weights(g - 1)
-                quantise_scores(3 + g)
-            nc.vector.quantize_mx(
-                out=g_codes_1[:, g, :, :].rearrange("p n i -> p (n i)").bitcast(FP8X4),
-                scales=g_scales_1[:, g, :, :].rearrange("p n i -> p (n i)"),
-                in_=gated[:].rearrange("p n i t -> p (n i t)"),
-            )
-            weights_T(g)
-            scores(4 + g)
-        quantise_weights(3)
-        quantise_scores(7)
-
-        for g in range(HID_PASSES):
-            for pair in range(2, 4):
-                gate_T(pair, g)
-            residual(nc.vector, g)
-            project(g)
-            if g == 0:
-                x_raw.append(load_residual(1))
-        for a in range(4, TOKEN_BLOCKS):
-            residual(nc.gpsimd, a)
-
-        for a in range(4, TOKEN_BLOCKS):
-            gated = work.tile([P, HID_PASSES, P, PACK], BF16, name="gated", tag="gated", align_bytes=64)
+        def project(a, half):
+            d_cols = slice(D_HALF * half, D_HALF * (half + 1))
+            bank = psum_tile(psum_v, ("pj", a, half), [P, D_HALF], F32)
             for g in range(HID_PASSES):
-                attend(g, a, gated[:, g, :, :])
-            nc.vector.quantize_mx(
-                out=g_codes_2[:, a - 4, :, :].rearrange("p g i -> p (g i)").bitcast(FP8X4),
-                scales=g_scales_2[:, a - 4, :, :].rearrange("p g i -> p (g i)"),
-                in_=gated[:].rearrange("p g i t -> p (g i t)"),
+                g_cols = slice(P * g, P * (g + 1))
+                nc.tensor.matmul_mx(
+                    out=bank[:],
+                    lhsT=g_codes[:, a, g_cols].bitcast(FP8X4),
+                    lhsT_scale=g_scales[:, a, g_cols],
+                    rhs=w_codes[:, g, d_cols].bitcast(FP8X4),
+                    rhs_scale=w_scales[:, g, d_cols],
+                    start=(g == 0),
+                    stop=(g == HID_PASSES - 1),
+                )
+
+        def finish(a, half):
+            d_cols = slice(D_HALF * half, D_HALF * (half + 1))
+            res = tiles[("rs", a)]
+            nc.vector.tensor_tensor(
+                out=res[:, d_cols], in0=tiles[("pj", a, half)][:], in1=res[:, d_cols], op=ALU.add
             )
-            if a > 4:
-                project(a - 1)
-        project(TOKEN_BLOCKS - 1)
+            nc.sync.dma_start(out=out_rows[:, a, d_cols], in_=res[:, d_cols])
+
+        def task(kind, i, engine):
+            copy = nc.scalar.copy if engine == "S" else nc.vector.tensor_copy
+            if kind == "ld":
+                what, n = i
+                buf = {"v": ("raw", 4), "W": ("raw", 4), "x": ("raw", 4), "g": ("gate", 4)}
+                return [], (buf[what] + (("ld", what, n),) if what in buf else None), [], lambda: load(what, n, nc.scalar if engine == "S" else nc.sync)
+            if kind == "T":
+                return [("ld", i[0], 0)], ("ps", 1, ("T",) + i), [], lambda: turn_qk(*i)
+            if kind == "C":
+                return [("T",) + i], None, [("T",) + i], lambda: keep_qk(i[0], i[1], copy)
+            if kind == "sc":
+                return [("C", "k", i[1]), ("C", "q", i[0] // 4)], ("ps", 1, ("sc",) + i), [], lambda: sim(*i)
+            if kind == "re":
+                opens = ("relu", 1, ("re", i[0])) if i[1] == 0 else None
+                return [("sc",) + i], opens, [("sc",) + i], lambda: relu(*i)
+            if kind == "sq":
+                return [("re", i[0], 0), ("re", i[0], 1)], ("a_grp", 1, ("sq",) + i), [("re",) + i], lambda: square(*i)
+            if kind == "qA":
+                return [("sq",) + i], None, [("sq",) + i], lambda: quantise_a(*i)
+            if kind == "vc":
+                opens = ("grp", 2, ("vg", i[0])) if ("vg", i[0]) not in left else None
+                return [("ld", "v", i[0])], opens, [("ld", "v", i[0])], lambda: group_v(i[0], i[1], i[2], copy)
+            if kind == "qv":
+                return [("vc",) + i + (0,), ("vc",) + i + (1,)], None, [("vg", i[0])], lambda: quantise_v(*i)
+            if kind == "av":
+                return [("qA", i[0]), ("qv", i[1], 0), ("qv", i[1], 1)], ("pv", 1, ("av",) + i), [], lambda: attend(*i)
+            if kind == "ga":
+                opens = ("gated", 1, ("ga", i[0], i[1] // 2)) if i[1] % 2 == 0 else None
+                return [("av",) + i, ("ld", "g", i[0])], opens, [("av",) + i, ("ld", "g", i[0])], lambda: apply_gate(*i)
+            if kind == "vt":
+                a, h = i
+                return [("ga", a, 2 * h), ("ga", a, 2 * h + 1)], ("ps", 1, ("vt",) + i), [("ga", a, h)], lambda: turn_v(*i)
+            if kind == "ve":
+                return [("vt",) + i], ("v_t", 1, ("ve",) + i), [("vt",) + i], lambda: keep_v(*i)
+            if kind == "qV":
+                return [("ve",) + i], None, [("ve",) + i], lambda: quantise_g(*i)
+            if kind == "wt":
+                return [("ld", "W", i[0])], ("ps", 1, ("wt",) + i), [("ld", "W", i[0])], lambda: turn_w(*i)
+            if kind == "we":
+                opens = ("grp", 2, ("wg", i[0])) if ("wg", i[0]) not in left else None
+                return [("wt",) + i], opens, [("wt",) + i], lambda: keep_w(*i)
+            if kind == "qW":
+                g, h = i
+                return [("we", g, 2 * h), ("we", g, 2 * h + 1)], None, [("wg", g)], lambda: quantise_w(*i)
+            if kind == "rs":
+                a = i[0]
+                return [("ld", "x", a // 4), ("ld", "b", 0)], ("resid", 2, ("rs", a)), [("ld", "x", a // 4)], lambda: residual(a)
+            if kind == "pj":
+                a, h = i
+                needs = [("qV", a, 0), ("qV", a, 1)] + [("qW", g, h) for g in range(HID_PASSES)]
+                return needs, ("pv", 1, ("pj",) + i), [], lambda: project(*i)
+            return [("pj",) + i, ("rs", i[0])], None, [("pj",) + i, ("rs", i[0])], lambda: finish(*i)
+
+        left = {}
+        rings = {name: [] for name in RING_BUFS}
+        done = set()
+        lanes = []
+        for engine, text in (("D", LOADS), ("P", TENSOR), ("S", SCALAR), ("V", VECTOR), ("G", GPSIMD)):
+            lane = []
+            for word in text.split():
+                parts = word.split(".")
+                lane.append((parts[0], tuple([n if n in ("k", "q", "v", "W", "g", "b", "x") else int(n) for n in parts[1:]])))
+            lanes.append([engine, lane, 0])
+        moved = True
+        while moved:
+            moved = False
+            for lane in lanes:
+                while lane[2] < len(lane[1]):
+                    kind, i = lane[1][lane[2]]
+                    needs, opens, reads, call = task(kind, i, lane[0])
+                    if not all([n in done for n in needs]):
+                        break
+                    if opens is not None:
+                        held = rings[opens[0]]
+                        if len(held) >= RING_BUFS[opens[0]] and left[held[-RING_BUFS[opens[0]]]] > 0:
+                            break
+                        held.append(opens[2])
+                        left[opens[2]] = opens[1]
+                    for key in reads:
+                        if key in left:
+                            left[key] -= 1
+                    call()
+                    done.add((kind,) + i)
+                    lane[2] += 1
+                    moved = True
+        assert all([lane[2] == len(lane[1]) for lane in lanes]), [lane[1][lane[2]] for lane in lanes if lane[2] < len(lane[1])]

@@ -25,29 +25,30 @@ D_HALF = 512
 
 FLOPS = 2 * S * S * QK + 2 * S * S * H + 2 * S * H * D
 
-LOADS = """ld.k.0 ld.q.0 ld.v.0 ld.v.1 ld.v.2 ld.g.0 ld.g.1 ld.v.3 ld.g.2 ld.g.3 ld.W.0 ld.W.1 ld.W.2 ld.W.3 ld.g.4
-ld.g.5 ld.b.0 ld.g.6 ld.g.7"""
+LOADS = """ld.k.0 ld.q.0 ld.v.0 ld.v.1 ld.b.0 ld.v.2 ld.g.0 ld.g.1 ld.v.3 ld.g.2 ld.W.0 ld.W.1 ld.g.3 ld.W.2 ld.W.3
+ld.g.4 ld.g.5 ld.g.6 ld.g.7"""
 TENSOR = """T.k.0 T.k.1 T.q.0 T.q.1 sc.0.0 sc.0.1 sc.1.0 sc.1.1 sc.2.0 sc.2.1 av.0.0 sc.3.0 sc.3.1 av.1.0 sc.4.0 sc.4.1
-av.2.0 av.0.1 av.1.1 sc.5.0 sc.5.1 av.2.1 vt.0.0 vt.1.0 wt.0.0 av.0.2 av.1.2 av.2.2 vt.2.0 wt.0.1 wt.0.2
-wt.0.3 av.0.3 av.1.3 av.2.3 wt.1.0 wt.1.1 av.3.0 av.3.1 vt.0.1 vt.1.1 wt.1.2 wt.1.3 av.3.2 av.3.3 vt.2.1
-wt.2.0 wt.2.1 sc.6.0 sc.6.1 av.4.0 av.4.1 vt.3.0 vt.3.1 wt.2.2 wt.2.3 wt.3.0 av.4.2 av.4.3 av.5.0 wt.3.1
-wt.3.2 wt.3.3 vt.4.0 vt.4.1 sc.7.0 sc.7.1 av.5.1 av.5.2 av.5.3 pj.0.0 pj.0.1 av.6.0 av.6.1 vt.5.0 vt.5.1
-pj.1.0 pj.1.1 av.6.2 av.6.3 pj.2.0 pj.2.1 vt.6.0 vt.6.1 av.7.0 av.7.1 pj.3.0 pj.3.1 av.7.2 av.7.3 pj.4.0
-pj.4.1 vt.7.0 vt.7.1 pj.5.0 pj.5.1 pj.6.0 pj.6.1 pj.7.0 pj.7.1"""
-SCALAR = """C.k.1 C.q.1 re.0.0 re.0.1 re.1.0 sq.0 re.1.1 re.2.0 sq.1 re.2.1 re.3.0 sq.2 re.3.1 re.4.0 sq.3 re.4.1 re.5.0
-sq.4 re.5.1 sq.5 ve.0.0 ve.1.0 we.0.0 ve.2.0 we.0.1 we.0.2 we.0.3 we.1.0 we.1.1 ve.0.1 ve.1.1 we.1.2 we.1.3
-ve.2.1 we.2.0 we.2.1 ld.x.0 re.6.0 re.6.1 ve.3.0 sq.6 ve.3.1 we.2.2 we.2.3 we.3.0 we.3.1 we.3.2 we.3.3 ve.4.0
-ve.4.1 ld.x.1 re.7.0 re.7.1 sq.7 ve.5.0 ve.5.1 ve.6.0 ve.6.1 ve.7.0 ve.7.1"""
+av.2.0 av.0.1 av.1.1 bb.0 bb.1 sc.5.0 sc.5.1 av.2.1 vt.0.0 vt.1.0 wt.0.0 av.0.2 av.1.2 av.2.2 vt.2.0 wt.1.0
+wt.2.0 wt.3.0 av.0.3 av.1.3 av.2.3 wt.0.1 wt.1.1 av.3.0 av.3.1 vt.0.1 vt.1.1 wt.2.1 wt.3.1 av.3.2 av.3.3
+vt.2.1 wt.0.2 wt.1.2 sc.6.0 sc.6.1 av.4.0 av.4.1 vt.3.0 vt.3.1 wt.2.2 wt.3.2 wt.0.3 av.4.2 av.4.3 av.5.0
+wt.1.3 wt.2.3 wt.3.3 vt.4.0 vt.4.1 sc.7.0 sc.7.1 av.5.1 av.5.2 av.5.3 pj.0.0 pj.0.1 av.6.0 av.6.1 vt.5.0
+vt.5.1 pj.1.0 pj.1.1 av.6.2 av.6.3 pj.2.0 pj.2.1 vt.6.0 vt.6.1 av.7.0 av.7.1 pj.3.0 pj.3.1 av.7.2 av.7.3
+pj.4.0 pj.4.1 vt.7.0 vt.7.1 pj.5.0 pj.5.1 pj.6.0 pj.6.1 pj.7.0 pj.7.1"""
+SCALAR = """C.k.1 C.q.1 re.0.0 re.0.1 re.1.0 sq.0 re.1.1 re.2.0 sq.1 re.2.1 re.3.0 sq.2 re.3.1 re.4.0 sq.3 re.4.1 bk.0
+bk.1 re.5.0 sq.4 re.5.1 sq.5 ve.0.0 ve.1.0 we.0.0 ve.2.0 we.1.0 we.2.0 we.3.0 we.0.1 we.1.1 ve.0.1 ve.1.1
+we.2.1 we.3.1 ve.2.1 ld.x.0 we.0.2 we.1.2 re.6.0 re.6.1 ve.3.0 sq.6 ve.3.1 we.2.2 we.3.2 we.0.3 we.1.3 we.2.3
+we.3.3 ve.4.0 ve.4.1 re.7.0 re.7.1 ld.x.1 sq.7 ve.5.0 ve.5.1 ve.6.0 ve.6.1 ve.7.0 ve.7.1"""
 VECTOR = """C.k.0 C.q.0 vc.0.0.0 vc.0.0.1 vc.0.1.0 vc.0.1.1 qv.0.0 qv.0.1 vc.1.0.0 qA.0 vc.1.0.1 vc.1.1.0 vc.1.1.1 qA.1
 qv.1.0 qv.1.1 vc.2.0.0 vc.2.0.1 ga.0.0 qA.2 vc.2.1.0 vc.2.1.1 ga.1.0 qv.2.0 ga.0.1 qv.2.1 ga.2.0 vc.3.0.0
 vc.3.0.1 ga.1.1 vc.3.1.0 vc.3.1.1 ga.2.1 qA.3 qv.3.0 qV.0.0 qv.3.1 qV.1.0 ga.0.2 qA.4 ga.1.2 qV.2.0 ga.2.2
-qW.0.0 ga.0.3 ga.1.3 qW.0.1 ga.2.3 ga.3.0 qA.5 ga.3.1 qV.0.1 qW.1.0 qV.1.1 ga.3.2 qW.1.1 qV.2.1 ga.3.3 ga.4.0
-ga.4.1 qW.2.0 qV.3.0 qV.3.1 ga.4.2 qW.2.1 ga.4.3 qA.6 ga.5.0 qW.3.0 qV.4.0 qV.4.1 ga.5.1 qW.3.1 ga.5.2 ga.5.3
-fi.0.0 fi.0.1 qA.7 ga.6.0 ga.6.1 qV.5.0 qV.5.1 fi.1.0 fi.1.1 ga.6.2 ga.6.3 fi.2.0 fi.2.1 qV.6.0 qV.6.1 ga.7.0
-ga.7.1 fi.3.0 fi.3.1 ga.7.2 ga.7.3 fi.4.0 fi.4.1 qV.7.0 qV.7.1 fi.5.0 fi.5.1 fi.6.0 fi.6.1 fi.7.0 fi.7.1"""
-GPSIMD = "rs.0 rs.1 rs.2 rs.3 rs.4 rs.5 rs.6 rs.7"
+ga.0.3 ga.1.3 ga.2.3 ga.3.0 qA.5 ga.3.1 qW.0.0 qV.0.1 qW.1.0 qV.1.1 ga.3.2 qW.2.0 qV.2.1 ga.3.3 qW.3.0 ga.4.0
+ga.4.1 qV.3.0 qV.3.1 ga.4.2 ga.4.3 qA.6 ga.5.0 qW.0.1 qW.1.1 ga.5.1 qV.4.0 qV.4.1 qW.2.1 ga.5.2 qW.3.1 ga.5.3
+fi.0.0 fi.0.1 qA.7 ga.6.0 ga.6.1 qV.5.0 qV.5.1 fi.1.0 fi.1.1 ga.6.2 ga.6.3 rs.4 fi.2.0 fi.2.1 qV.6.0 qV.6.1
+ga.7.0 ga.7.1 rs.5 fi.3.0 fi.3.1 ga.7.2 ga.7.3 fi.4.0 fi.4.1 rs.6 qV.7.0 qV.7.1 fi.5.0 fi.5.1 rs.7 fi.6.0
+fi.6.1 fi.7.0 fi.7.1"""
+GPSIMD = "rs.0 rs.1 rs.2 rs.3"
 
-RING_BUFS = {"raw":5,"gate":6,"relu":3,"a_grp":4,"grp":2,"gated":8,"v_t":4,"resid":4,"ps":4,"pv":4}
+RING_BUFS = {"raw":5,"gate":6,"relu":3,"a_grp":4,"grp":5,"gated":8,"v_t":4,"resid":4,"ps":4,"pv":4}
 
 
 def tile_gau_pa_kernel(tc, q, k, v, gate, W_out, b_out, x, out):
@@ -83,6 +84,10 @@ def tile_gau_pa_kernel(tc, q, k, v, gate, W_out, b_out, x, out):
         g_scales = keep.tile([P, BLOCKS, HID_PASSES * P], U8, name="g_scales", align_bytes=64)
         make_identity(nc, ident_bf[:])
         make_identity(nc, ident_f32[:])
+        b_row = keep.tile([P, D], BF16, name="b_row")
+        nc.gpsimd.memset(b_row[:], 0.0)
+        ones = keep.tile([P, P], BF16, name="ones")
+        nc.gpsimd.memset(ones[:], 1.0)
 
         tiles = {}
 
@@ -103,7 +108,7 @@ def tile_gau_pa_kernel(tc, q, k, v, gate, W_out, b_out, x, out):
             elif what == "q":
                 nc.sync.dma_start(out=q_sb[:], in_=q_rows.rearrange("(p a) d -> p a d", a=BLOCKS))
             elif what == "b":
-                nc.sync.dma_start(out=bias_all[:], in_=b_out.partition_broadcast(P))
+                nc.sync.dma_start(out=b_row[0:1, :], in_=b_out.rearrange("(o d) -> o d", o=1))
             elif what == "v":
                 raw = ring_tile("raw", ("v", i), [P, KEY_PASSES * PACK * K_PASS], BF16)
                 view = raw[:].rearrange("p (c t h) -> p c t h", c=KEY_PASSES, t=PACK)
@@ -118,10 +123,10 @@ def tile_gau_pa_kernel(tc, q, k, v, gate, W_out, b_out, x, out):
                 raw = ring_tile("gate", ("g", i), [P, H], BF16)
                 nc.sync.dma_start(out=raw[:], in_=gate_rows[:, i, :])
             elif what == "W":
-                raw = ring_tile("raw", ("W", i), [P, (D // P) * K_PASS], BF16)
+                raw = ring_tile("raw", ("W", i), [P, 2 * H], BF16)
                 nc.sync.dma_start(
-                    out=raw[:].rearrange("p (a h) -> p a h", a=D // P),
-                    in_=W_out[:, K_PASS * i : K_PASS * (i + 1)].rearrange("(a p) h -> p a h", p=P),
+                    out=raw[:].rearrange("p (n h) -> p n h", n=2),
+                    in_=W_out[2 * P * i : 2 * P * (i + 1), :].rearrange("(n p) h -> p n h", p=P),
                 )
             else:
                 raw = ring_tile("raw", ("x", i), [P, 4 * D], BF16)
@@ -138,6 +143,15 @@ def tile_gau_pa_kernel(tc, q, k, v, gate, W_out, b_out, x, out):
         def keep_qk(what, half, copy):
             dst = kT if what == "k" else qT
             copy(out=dst[:, 4 * half : 4 * half + 4, :], in_=tiles[("T" + what, half)][:])
+
+        def spread_bias(half):
+            bank = psum_tile(psum_s, ("bb", half), [P, D_HALF], F32)
+            cols = slice(D_HALF * half, D_HALF * (half + 1))
+            nc.tensor.matmul(out=bank[:], lhsT=ones[:], rhs=b_row[:, cols], start=True, stop=True)
+
+        def keep_bias(half):
+            cols = slice(D_HALF * half, D_HALF * (half + 1))
+            nc.scalar.copy(out=bias_all[:, cols], in_=tiles[("bb", half)][:])
 
         def sim(a, c):
             bank = psum_tile(psum_s, ("sc", a, c), [P, PACK, P], F32)
@@ -168,17 +182,17 @@ def tile_gau_pa_kernel(tc, q, k, v, gate, W_out, b_out, x, out):
             )
 
         def group_v(g, c, half, copy):
-            if ("vg", g) not in tiles:
-                ring_tile("grp", ("vg", g), [P, KEY_PASSES, K_PASS * PACK], BF16)
+            if ("vg", g, c) not in tiles:
+                ring_tile("grp", ("vg", g, c), [P, K_PASS * PACK], BF16)
             src = tiles[("v", g)][:].rearrange("p (c t n i) -> p c n t i", c=KEY_PASSES, t=PACK, i=4)
-            dst = tiles[("vg", g)][:].rearrange("p c (n i t) -> p c n t i", i=4, t=PACK)
+            dst = tiles[("vg", g, c)][:].rearrange("p (n i t) -> p n t i", i=4, t=PACK)
             rows = slice(64 * half, 64 * half + 64)
-            copy(out=dst[:, c, rows, :, :], in_=src[:, c, rows, :, :])
+            copy(out=dst[:, rows, :, :], in_=src[:, c, rows, :, :])
 
         def quantise_v(g, c):
             cols = slice(K_PASS * c, K_PASS * (c + 1))
             nc.vector.quantize_mx(
-                out=v_codes[:, g, cols].bitcast(FP8X4), scales=v_scales[:, g, cols], in_=tiles[("vg", g)][:, c, :]
+                out=v_codes[:, g, cols].bitcast(FP8X4), scales=v_scales[:, g, cols], in_=tiles[("vg", g, c)][:]
             )
 
         def attend(a, g):
@@ -207,15 +221,15 @@ def tile_gau_pa_kernel(tc, q, k, v, gate, W_out, b_out, x, out):
                 op=ALU.mult,
             )
 
-        def turn_words(key, words):
+        def turn_words(key, words, first_words):
             bank = psum_tile(psum_s, key, [P, 2, 2, P], F32)
             for n in range(2):
                 for u in range(2):
-                    first = 2 * P * n + P * u
+                    first = first_words[n] + P * u
                     nc.tensor.transpose(bank[:, n, u, :], words[:, first : first + P], ident_f32[:])
 
         def turn_v(a, h):
-            turn_words(("vt", a, h), tiles[("ga", a, h)][:].bitcast(F32))
+            turn_words(("vt", a, h), tiles[("ga", a, h)][:].bitcast(F32), (0, 2 * P))
 
         def keep_v(a, h):
             grp = ring_tile("v_t", ("ve", a, h), [P, 2 * K_PASS], BF16)
@@ -231,16 +245,15 @@ def tile_gau_pa_kernel(tc, q, k, v, gate, W_out, b_out, x, out):
             )
 
         def turn_w(g, pair):
-            words = tiles[("W", g)][:].bitcast(F32)
-            turn_words(("wt", g, pair), words[:, 4 * P * pair : 4 * P * (pair + 1)])
+            turn_words(("wt", g, pair), tiles[("W", pair)][:].bitcast(F32), [(H // 2) * n + 2 * P * g for n in range(2)])
 
         def keep_w(g, pair):
-            if ("wg", g) not in tiles:
-                ring_tile("grp", ("wg", g), [P, KEY_PASSES, K_PASS * PACK], BF16)
-            dst = tiles[("wg", g)][:].rearrange("p c w -> p (c w)").bitcast(F32)
-            dst = dst.rearrange("p (n r u) -> p n r u", n=D // P, u=2)
+            half = pair // 2
+            if ("wg", g, half) not in tiles:
+                ring_tile("grp", ("wg", g, half), [P, D_HALF * PACK], BF16)
+            dst = tiles[("wg", g, half)][:].bitcast(F32).rearrange("p (n r u) -> p n r u", n=4, u=2)
             nc.scalar.copy(
-                out=dst[:, 2 * pair : 2 * pair + 2, :, :],
+                out=dst[:, 2 * (pair % 2) : 2 * (pair % 2) + 2, :, :],
                 in_=tiles[("wt", g, pair)][:].rearrange("p n u r -> p n r u"),
             )
 
@@ -249,15 +262,15 @@ def tile_gau_pa_kernel(tc, q, k, v, gate, W_out, b_out, x, out):
             nc.vector.quantize_mx(
                 out=w_codes[:, g, cols].bitcast(FP8X4),
                 scales=w_scales[:, g, cols],
-                in_=tiles[("wg", g)][:, half, :],
+                in_=tiles[("wg", g, half)][:],
             )
 
-        def residual(a):
+        def residual(a, engine, pieces):
             res = ring_tile("resid", ("rs", a), [P, D], F32)
-            for n in range(4):
-                cols = slice(256 * n, 256 * (n + 1))
+            for n in range(pieces):
+                cols = slice(D // pieces * n, D // pieces * (n + 1))
                 x_view = tiles[("x", a // 4)][:].rearrange("p (a d) -> p a d", a=4)
-                nc.gpsimd.tensor_tensor(
+                engine.tensor_tensor(
                     out=res[:, cols], in0=x_view[:, a % 4, cols], in1=bias_all[:, cols], op=ALU.add
                 )
 
@@ -294,6 +307,10 @@ def tile_gau_pa_kernel(tc, q, k, v, gate, W_out, b_out, x, out):
                 return [("ld", i[0], 0)], ("ps", 1, ("T",) + i), [], lambda: turn_qk(*i)
             if kind == "C":
                 return [("T",) + i], None, [("T",) + i], lambda: keep_qk(i[0], i[1], copy)
+            if kind == "bb":
+                return [("ld", "b", 0)], ("ps", 1, ("bb",) + i), [], lambda: spread_bias(*i)
+            if kind == "bk":
+                return [("bb",) + i], None, [("bb",) + i], lambda: keep_bias(*i)
             if kind == "sc":
                 return [("C", "k", i[1]), ("C", "q", i[0] // 4)], ("ps", 1, ("sc",) + i), [], lambda: sim(*i)
             if kind == "re":
@@ -304,10 +321,10 @@ def tile_gau_pa_kernel(tc, q, k, v, gate, W_out, b_out, x, out):
             if kind == "qA":
                 return [("sq",) + i], None, [("sq",) + i], lambda: quantise_a(*i)
             if kind == "vc":
-                opens = ("grp", 2, ("vg", i[0])) if ("vg", i[0]) not in left else None
+                opens = ("grp", 1, ("vg",) + i[:2]) if ("vg",) + i[:2] not in left else None
                 return [("ld", "v", i[0])], opens, [("ld", "v", i[0])], lambda: group_v(i[0], i[1], i[2], copy)
             if kind == "qv":
-                return [("vc",) + i + (0,), ("vc",) + i + (1,)], None, [("vg", i[0])], lambda: quantise_v(*i)
+                return [("vc",) + i + (0,), ("vc",) + i + (1,)], None, [("vg",) + i], lambda: quantise_v(*i)
             if kind == "av":
                 return [("qA", i[0]), ("qv", i[1], 0), ("qv", i[1], 1)], ("pv", 1, ("av",) + i), [], lambda: attend(*i)
             if kind == "ga":
@@ -321,16 +338,19 @@ def tile_gau_pa_kernel(tc, q, k, v, gate, W_out, b_out, x, out):
             if kind == "qV":
                 return [("ve",) + i], None, [("ve",) + i], lambda: quantise_g(*i)
             if kind == "wt":
-                return [("ld", "W", i[0])], ("ps", 1, ("wt",) + i), [("ld", "W", i[0])], lambda: turn_w(*i)
+                return [("ld", "W", i[1])], ("ps", 1, ("wt",) + i), [("ld", "W", i[1])], lambda: turn_w(*i)
             if kind == "we":
-                opens = ("grp", 2, ("wg", i[0])) if ("wg", i[0]) not in left else None
+                key = ("wg", i[0], i[1] // 2)
+                opens = ("grp", 1, key) if key not in left else None
                 return [("wt",) + i], opens, [("wt",) + i], lambda: keep_w(*i)
             if kind == "qW":
                 g, h = i
-                return [("we", g, 2 * h), ("we", g, 2 * h + 1)], None, [("wg", g)], lambda: quantise_w(*i)
+                return [("we", g, 2 * h), ("we", g, 2 * h + 1)], None, [("wg", g, h)], lambda: quantise_w(*i)
             if kind == "rs":
                 a = i[0]
-                return [("ld", "x", a // 4), ("ld", "b", 0)], ("resid", 2, ("rs", a)), [("ld", "x", a // 4)], lambda: residual(a)
+                where = (nc.vector, 1) if engine == "V" else (nc.gpsimd, 4)
+                needs = [("ld", "x", a // 4), ("bk", 0), ("bk", 1)]
+                return needs, ("resid", 2, ("rs", a)), [("ld", "x", a // 4)], lambda: residual(a, *where)
             if kind == "pj":
                 a, h = i
                 needs = [("qV", a, 0), ("qV", a, 1)] + [("qW", g, h) for g in range(HID_PASSES)]

@@ -25,24 +25,24 @@ D_HALF = 512
 
 FLOPS = 2 * S * S * QK + 2 * S * S * H + 2 * S * H * D
 
-LOADS = """ld.k.0 ld.q.0 ld.v.0 ld.v.1 ld.b.0 ld.v.2 ld.g.0 ld.g.1 ld.v.3 ld.g.2 ld.W.0 ld.W.1 ld.g.3 ld.W.2 ld.W.3
-ld.g.4 ld.g.5 ld.g.6 ld.g.7"""
-TENSOR = """T.k.0 T.k.1 T.q.0 T.q.1 sc.0.0 sc.0.1 sc.1.0 sc.1.1 sc.2.0 sc.2.1 av.0.0 sc.3.0 sc.3.1 av.1.0 sc.4.0 sc.4.1
+LOADS = """ld.k.0 ld.q.0 ld.v.0.0 ld.k.1 ld.v.0.1 ld.q.1 ld.v.1.0 ld.v.1.1 ld.b.0 ld.v.2.0 ld.v.2.1 ld.g.0 ld.g.1
+ld.v.3.0 ld.v.3.1 ld.g.2 ld.W.0 ld.W.1 ld.g.3 ld.W.2 ld.W.3 ld.g.4 ld.g.5 ld.g.6 ld.g.7"""
+TENSOR = """T.k.0 T.q.0 T.k.1 sc.0.0 sc.0.1 sc.1.0 sc.1.1 sc.2.0 sc.2.1 av.0.0 sc.3.0 sc.3.1 av.1.0 T.q.1 sc.4.0 sc.4.1
 av.2.0 av.0.1 av.1.1 bb.0 bb.1 sc.5.0 sc.5.1 av.2.1 vt.0.0 vt.1.0 wt.0.0 av.0.2 av.1.2 av.2.2 vt.2.0 wt.1.0
 wt.2.0 wt.3.0 av.0.3 av.1.3 av.2.3 wt.0.1 wt.1.1 av.3.0 av.3.1 vt.0.1 vt.1.1 wt.2.1 wt.3.1 av.3.2 av.3.3
 vt.2.1 wt.0.2 wt.1.2 sc.6.0 sc.6.1 av.4.0 av.4.1 vt.3.0 vt.3.1 wt.2.2 wt.3.2 wt.0.3 av.4.2 av.4.3 av.5.0
-wt.1.3 wt.2.3 wt.3.3 vt.4.0 vt.4.1 sc.7.0 sc.7.1 av.5.1 av.5.2 av.5.3 pj.0.0 pj.0.1 av.6.0 av.6.1 vt.5.0
+av.5.1 wt.1.3 wt.2.3 wt.3.3 vt.4.0 vt.4.1 sc.7.0 sc.7.1 av.5.2 av.5.3 pj.0.0 pj.0.1 av.6.0 av.6.1 vt.5.0
 vt.5.1 pj.1.0 pj.1.1 av.6.2 av.6.3 pj.2.0 pj.2.1 vt.6.0 vt.6.1 av.7.0 av.7.1 pj.3.0 pj.3.1 av.7.2 av.7.3
 pj.4.0 pj.4.1 vt.7.0 vt.7.1 pj.5.0 pj.5.1 pj.6.0 pj.6.1 pj.7.0 pj.7.1"""
-SCALAR = """C.k.1 C.q.1 re.0.0 re.0.1 re.1.0 sq.0 re.1.1 re.2.0 sq.1 re.2.1 re.3.0 sq.2 re.3.1 re.4.0 sq.3 re.4.1 bk.0
+SCALAR = """C.k.1 re.0.0 re.0.1 re.1.0 sq.0 re.1.1 re.2.0 sq.1 re.2.1 re.3.0 sq.2 C.q.1 re.3.1 re.4.0 sq.3 re.4.1 bk.0
 bk.1 re.5.0 sq.4 re.5.1 sq.5 ve.0.0 ve.1.0 we.0.0 ve.2.0 we.1.0 we.2.0 we.3.0 we.0.1 we.1.1 ve.0.1 ve.1.1
-we.2.1 we.3.1 ve.2.1 ld.x.0 we.0.2 we.1.2 re.6.0 re.6.1 ve.3.0 sq.6 ve.3.1 we.2.2 we.3.2 we.0.3 we.1.3 we.2.3
+we.2.1 we.3.1 ve.2.1 we.0.2 we.1.2 re.6.0 re.6.1 ve.3.0 ve.3.1 sq.6 ld.x.0 we.2.2 we.3.2 we.0.3 we.1.3 we.2.3
 we.3.3 ve.4.0 ve.4.1 re.7.0 re.7.1 ld.x.1 sq.7 ve.5.0 ve.5.1 ve.6.0 ve.6.1 ve.7.0 ve.7.1"""
 VECTOR = """C.k.0 C.q.0 vc.0.0.0 vc.0.0.1 vc.0.1.0 vc.0.1.1 qv.0.0 qv.0.1 vc.1.0.0 qA.0 vc.1.0.1 vc.1.1.0 vc.1.1.1 qA.1
 qv.1.0 qv.1.1 vc.2.0.0 vc.2.0.1 ga.0.0 qA.2 vc.2.1.0 vc.2.1.1 ga.1.0 qv.2.0 ga.0.1 qv.2.1 ga.2.0 vc.3.0.0
 vc.3.0.1 ga.1.1 vc.3.1.0 vc.3.1.1 ga.2.1 qA.3 qv.3.0 qV.0.0 qv.3.1 qV.1.0 ga.0.2 qA.4 ga.1.2 qV.2.0 ga.2.2
 ga.0.3 ga.1.3 ga.2.3 ga.3.0 qA.5 ga.3.1 qW.0.0 qV.0.1 qW.1.0 qV.1.1 ga.3.2 qW.2.0 qV.2.1 ga.3.3 qW.3.0 ga.4.0
-ga.4.1 qV.3.0 qV.3.1 ga.4.2 ga.4.3 qA.6 ga.5.0 qW.0.1 qW.1.1 ga.5.1 qV.4.0 qV.4.1 qW.2.1 ga.5.2 qW.3.1 ga.5.3
+ga.4.1 qV.3.0 qV.3.1 ga.4.2 ga.4.3 qA.6 ga.5.0 qW.0.1 qW.1.1 ga.5.1 qW.2.1 ga.5.2 qW.3.1 qV.4.0 qV.4.1 ga.5.3
 fi.0.0 fi.0.1 qA.7 ga.6.0 ga.6.1 qV.5.0 qV.5.1 fi.1.0 fi.1.1 ga.6.2 ga.6.3 rs.4 fi.2.0 fi.2.1 qV.6.0 qV.6.1
 ga.7.0 ga.7.1 rs.5 fi.3.0 fi.3.1 ga.7.2 ga.7.3 fi.4.0 fi.4.1 rs.6 qV.7.0 qV.7.1 fi.5.0 fi.5.1 rs.7 fi.6.0
 fi.6.1 fi.7.0 fi.7.1"""
@@ -99,26 +99,29 @@ def tile_gau_pa_kernel(tc, q, k, v, gate, W_out, b_out, x, out):
             tiles[key] = pool.tile(shape, dtype, name="bank", tag="bank")
             return tiles[key]
 
-        def load(what, i, queue):
+        def load(what, i, c, queue):
             if what == "k":
                 nc.sync.dma_start(
-                    out=k_sb[:].rearrange("p (c t) d -> p c t d", c=KEY_PASSES),
-                    in_=k_rows.rearrange("(c p t) d -> p c t d", c=KEY_PASSES, t=PACK),
+                    out=k_sb[:, PACK * i : PACK * (i + 1), :],
+                    in_=k_rows[K_PASS * i : K_PASS * (i + 1), :].rearrange("(p t) d -> p t d", t=PACK),
                 )
             elif what == "q":
-                nc.sync.dma_start(out=q_sb[:], in_=q_rows.rearrange("(p a) d -> p a d", a=BLOCKS))
+                nc.sync.dma_start(
+                    out=q_sb[:, 4 * i : 4 * i + 4, :],
+                    in_=q_rows.rearrange("(p a) d -> p a d", a=BLOCKS)[:, 4 * i : 4 * i + 4, :],
+                )
             elif what == "b":
                 nc.sync.dma_start(out=b_row[0:1, :], in_=b_out.rearrange("(o d) -> o d", o=1))
             elif what == "v":
-                raw = ring_tile("raw", ("v", i), [P, KEY_PASSES * PACK * K_PASS], BF16)
-                view = raw[:].rearrange("p (c t h) -> p c t h", c=KEY_PASSES, t=PACK)
-                for c in range(KEY_PASSES):
-                    nc.sync.dma_start(
-                        out=view[:, c, :, :],
-                        in_=v_rows[K_PASS * c : K_PASS * (c + 1), K_PASS * i : K_PASS * (i + 1)].rearrange(
-                            "(p t) h -> p t h", t=PACK
-                        ),
-                    )
+                if ("v", i) not in tiles:
+                    ring_tile("raw", ("v", i), [P, KEY_PASSES * PACK * K_PASS], BF16)
+                view = tiles[("v", i)][:].rearrange("p (c t h) -> p c t h", c=KEY_PASSES, t=PACK)
+                nc.sync.dma_start(
+                    out=view[:, c, :, :],
+                    in_=v_rows[K_PASS * c : K_PASS * (c + 1), K_PASS * i : K_PASS * (i + 1)].rearrange(
+                        "(p t) h -> p t h", t=PACK
+                    ),
+                )
             elif what == "g":
                 raw = ring_tile("gate", ("g", i), [P, H], BF16)
                 nc.sync.dma_start(out=raw[:], in_=gate_rows[:, i, :])
@@ -289,6 +292,29 @@ def tile_gau_pa_kernel(tc, q, k, v, gate, W_out, b_out, x, out):
                     stop=(g == HID_PASSES - 1),
                 )
 
+        def project_piece(a, piece):
+            d_cols = slice(D // 4 * piece, D // 4 * (piece + 1))
+            bank = psum_tile(psum_v, ("pq", a, piece), [P, D // 4], F32)
+            for g in range(HID_PASSES):
+                g_cols = slice(P * g, P * (g + 1))
+                nc.tensor.matmul_mx(
+                    out=bank[:],
+                    lhsT=g_codes[:, a, g_cols].bitcast(FP8X4),
+                    lhsT_scale=g_scales[:, a, g_cols],
+                    rhs=w_codes[:, g, d_cols].bitcast(FP8X4),
+                    rhs_scale=w_scales[:, g, d_cols],
+                    start=(g == 0),
+                    stop=(g == HID_PASSES - 1),
+                )
+
+        def finish_piece(a, piece):
+            d_cols = slice(D // 4 * piece, D // 4 * (piece + 1))
+            res = tiles[("rs", a)]
+            nc.vector.tensor_tensor(
+                out=res[:, d_cols], in0=tiles[("pq", a, piece)][:], in1=res[:, d_cols], op=ALU.add
+            )
+            nc.sync.dma_start(out=out_rows[:, a, d_cols], in_=res[:, d_cols])
+
         def finish(a, half):
             d_cols = slice(D_HALF * half, D_HALF * (half + 1))
             res = tiles[("rs", a)]
@@ -297,14 +323,31 @@ def tile_gau_pa_kernel(tc, q, k, v, gate, W_out, b_out, x, out):
             )
             nc.sync.dma_start(out=out_rows[:, a, d_cols], in_=res[:, d_cols])
 
+        def add_residual(a, half):
+            d_cols = slice(D_HALF * half, D_HALF * (half + 1))
+            if half == 0:
+                ring_tile("resid", ("rs", a), [P, D], F32)
+            x_view = tiles[("x", a // 4)][:].rearrange("p (a d) -> p a d", a=4)
+            nc.vector.tensor_tensor(
+                out=tiles[("rs", a)][:, d_cols], in0=tiles[("pj", a, half)][:], in1=x_view[:, a % 4, d_cols], op=ALU.add
+            )
+
+        def add_bias(a, half):
+            d_cols = slice(D_HALF * half, D_HALF * (half + 1))
+            res = tiles[("rs", a)]
+            nc.gpsimd.tensor_tensor(out=res[:, d_cols], in0=res[:, d_cols], in1=bias_all[:, d_cols], op=ALU.add)
+            nc.sync.dma_start(out=out_rows[:, a, d_cols], in_=res[:, d_cols])
+
         def task(kind, i, engine):
             copy = nc.scalar.copy if engine == "S" else nc.vector.tensor_copy
             if kind == "ld":
-                what, n = i
+                what, n = i[:2]
+                c = i[2] if what == "v" else 0
                 buf = {"v": ("raw", 4), "W": ("raw", 4), "x": ("raw", 4), "g": ("gate", 4)}
-                return [], (buf[what] + (("ld", what, n),) if what in buf else None), [], lambda: load(what, n, nc.scalar if engine == "S" else nc.sync)
+                opens = buf[what] + (("ld", what, n),) if what in buf and ("ld", what, n) not in left else None
+                return [], opens, [], lambda: load(what, n, c, nc.scalar if engine == "S" else nc.sync)
             if kind == "T":
-                return [("ld", i[0], 0)], ("ps", 1, ("T",) + i), [], lambda: turn_qk(*i)
+                return [("ld",) + i], ("ps", 1, ("T",) + i), [], lambda: turn_qk(*i)
             if kind == "C":
                 return [("T",) + i], None, [("T",) + i], lambda: keep_qk(i[0], i[1], copy)
             if kind == "bb":
@@ -322,7 +365,7 @@ def tile_gau_pa_kernel(tc, q, k, v, gate, W_out, b_out, x, out):
                 return [("sq",) + i], None, [("sq",) + i], lambda: quantise_a(*i)
             if kind == "vc":
                 opens = ("grp", 1, ("vg",) + i[:2]) if ("vg",) + i[:2] not in left else None
-                return [("ld", "v", i[0])], opens, [("ld", "v", i[0])], lambda: group_v(i[0], i[1], i[2], copy)
+                return [("ld", "v", i[0], i[1])], opens, [("ld", "v", i[0])], lambda: group_v(i[0], i[1], i[2], copy)
             if kind == "qv":
                 return [("vc",) + i + (0,), ("vc",) + i + (1,)], None, [("vg",) + i], lambda: quantise_v(*i)
             if kind == "av":
@@ -355,6 +398,17 @@ def tile_gau_pa_kernel(tc, q, k, v, gate, W_out, b_out, x, out):
                 a, h = i
                 needs = [("qV", a, 0), ("qV", a, 1)] + [("qW", g, h) for g in range(HID_PASSES)]
                 return needs, ("pv", 1, ("pj",) + i), [], lambda: project(*i)
+            if kind == "pq":
+                a, n = i
+                needs = [("qV", a, 0), ("qV", a, 1)] + [("qW", g, n // 2) for g in range(HID_PASSES)]
+                return needs, ("pv", 1, ("pq",) + i), [], lambda: project_piece(*i)
+            if kind == "fq":
+                return [("pq",) + i, ("rs", i[0])], None, [("pq",) + i, ("rs", i[0])], lambda: finish_piece(*i)
+            if kind == "fx":
+                opens = ("resid", 2, ("rs", i[0])) if i[1] == 0 else None
+                return [("pj",) + i, ("ld", "x", i[0] // 4)], opens, [("pj",) + i, ("ld", "x", i[0] // 4)], lambda: add_residual(*i)
+            if kind == "gb":
+                return [("fx",) + i, ("bk", 0), ("bk", 1)], None, [("rs", i[0])], lambda: add_bias(*i)
             return [("pj",) + i, ("rs", i[0])], None, [("pj",) + i, ("rs", i[0])], lambda: finish(*i)
 
         left = {}

@@ -29,23 +29,23 @@ LOADS = """ld.k.0 ld.q.0 ld.v.0.0 ld.k.1 ld.v.0.1 ld.q.1 ld.v.1.0 ld.v.1.1 ld.b.
 ld.v.3.0 ld.v.3.1 ld.g.2 ld.W.0 ld.W.1 ld.g.3 ld.W.2 ld.W.3 ld.g.4 ld.g.5 ld.g.6 ld.g.7"""
 TENSOR = """T.k.0 T.q.0 T.k.1 sc.0.0 sc.0.1 sc.1.0 sc.1.1 sc.2.0 sc.2.1 av.0.0 sc.3.0 sc.3.1 av.1.0 T.q.1 sc.4.0 sc.4.1
 av.2.0 av.0.1 av.1.1 bb.0 bb.1 sc.5.0 sc.5.1 av.2.1 vt.0.0 vt.1.0 wt.0.0 av.0.2 av.1.2 av.2.2 vt.2.0 wt.1.0
-wt.2.0 wt.3.0 av.0.3 av.1.3 av.2.3 wt.0.1 wt.1.1 av.3.0 av.3.1 vt.0.1 vt.1.1 wt.2.1 wt.3.1 av.3.2 av.3.3
+wt.2.0 wt.3.0 av.0.3 wt.0.1 wt.1.1 av.1.3 av.2.3 av.3.0 av.3.1 vt.0.1 vt.1.1 wt.2.1 wt.3.1 av.3.2 av.3.3
 vt.2.1 wt.0.2 wt.1.2 sc.6.0 sc.6.1 av.4.0 av.4.1 vt.3.0 vt.3.1 wt.2.2 wt.3.2 wt.0.3 av.4.2 av.4.3 av.5.0
-av.5.1 wt.1.3 wt.2.3 wt.3.3 vt.4.0 vt.4.1 sc.7.0 sc.7.1 av.5.2 av.5.3 pj.0.0 pj.0.1 av.6.0 av.6.1 vt.5.0
+av.5.1 wt.1.3 wt.2.3 wt.3.3 av.5.2 vt.4.0 vt.4.1 sc.7.0 sc.7.1 av.5.3 pj.0.0 pj.0.1 av.6.0 av.6.1 vt.5.0
 vt.5.1 pj.1.0 pj.1.1 av.6.2 av.6.3 pj.2.0 pj.2.1 vt.6.0 vt.6.1 av.7.0 av.7.1 pj.3.0 pj.3.1 av.7.2 av.7.3
-pj.4.0 pj.4.1 vt.7.0 vt.7.1 pj.5.0 pj.5.1 pj.6.0 pj.6.1 pj.7.0 pj.7.1"""
+pj.4.0 pj.4.1 vt.7.0 vt.7.1 pj.5.0 pj.5.1 pj.6.0 pj.6.1 pj.7.0 pq.7.2 pq.7.3"""
 SCALAR = """C.k.1 re.0.0 re.0.1 re.1.0 sq.0 re.1.1 re.2.0 sq.1 re.2.1 re.3.0 sq.2 C.q.1 re.3.1 re.4.0 sq.3 re.4.1 bk.0
 bk.1 re.5.0 sq.4 re.5.1 sq.5 ve.0.0 ve.1.0 we.0.0 ve.2.0 we.1.0 we.2.0 we.3.0 we.0.1 we.1.1 ve.0.1 ve.1.1
 we.2.1 we.3.1 ve.2.1 we.0.2 we.1.2 re.6.0 re.6.1 ve.3.0 ve.3.1 sq.6 ld.x.0 we.2.2 we.3.2 we.0.3 we.1.3 we.2.3
 we.3.3 ve.4.0 ve.4.1 re.7.0 re.7.1 ld.x.1 sq.7 ve.5.0 ve.5.1 ve.6.0 ve.6.1 ve.7.0 ve.7.1"""
-VECTOR = """C.k.0 C.q.0 vc.0.0.0 vc.0.0.1 vc.0.1.0 vc.0.1.1 qv.0.0 qv.0.1 vc.1.0.0 qA.0 vc.1.0.1 vc.1.1.0 vc.1.1.1 qA.1
-qv.1.0 qv.1.1 vc.2.0.0 vc.2.0.1 ga.0.0 qA.2 vc.2.1.0 vc.2.1.1 ga.1.0 qv.2.0 ga.0.1 qv.2.1 ga.2.0 vc.3.0.0
+VECTOR = """C.k.0 C.q.0 vc.0.0.0 vc.0.0.1 vc.0.1.0 vc.0.1.1 qv.0.0 qv.0.1 vc.1.0.0 qA.0 vc.1.0.1 vc.1.1.0 vc.1.1.1 qv.1.0
+qA.1 qv.1.1 vc.2.0.0 vc.2.0.1 ga.0.0 qA.2 vc.2.1.0 vc.2.1.1 ga.1.0 qv.2.0 ga.0.1 qv.2.1 ga.2.0 vc.3.0.0
 vc.3.0.1 ga.1.1 vc.3.1.0 vc.3.1.1 ga.2.1 qA.3 qv.3.0 qV.0.0 qv.3.1 qV.1.0 ga.0.2 qA.4 ga.1.2 qV.2.0 ga.2.2
 ga.0.3 ga.1.3 ga.2.3 ga.3.0 qA.5 ga.3.1 qW.0.0 qV.0.1 qW.1.0 qV.1.1 ga.3.2 qW.2.0 qV.2.1 ga.3.3 qW.3.0 ga.4.0
 ga.4.1 qV.3.0 qV.3.1 ga.4.2 ga.4.3 qA.6 ga.5.0 qW.0.1 qW.1.1 ga.5.1 qW.2.1 ga.5.2 qW.3.1 qV.4.0 qV.4.1 ga.5.3
 fi.0.0 fi.0.1 qA.7 ga.6.0 ga.6.1 qV.5.0 qV.5.1 fi.1.0 fi.1.1 ga.6.2 ga.6.3 rs.4 fi.2.0 fi.2.1 qV.6.0 qV.6.1
-ga.7.0 ga.7.1 rs.5 fi.3.0 fi.3.1 ga.7.2 ga.7.3 fi.4.0 fi.4.1 rs.6 qV.7.0 qV.7.1 fi.5.0 fi.5.1 rs.7 fi.6.0
-fi.6.1 fi.7.0 fi.7.1"""
+ga.7.0 ga.7.1 fi.3.0 fi.3.1 rs.5 ga.7.2 ga.7.3 fi.4.0 fi.4.1 rs.6 qV.7.0 qV.7.1 fi.5.0 fi.5.1 rs.7 fi.6.0
+fi.6.1 fi.7.0 fq.7.2 fq.7.3"""
 GPSIMD = "rs.0 rs.1 rs.2 rs.3"
 
 RING_BUFS = {"raw":5,"gate":6,"relu":3,"a_grp":4,"grp":5,"gated":8,"v_t":4,"resid":4,"ps":4,"pv":4}
@@ -85,9 +85,9 @@ def tile_gau_pa_kernel(tc, q, k, v, gate, W_out, b_out, x, out):
         make_identity(nc, ident_bf[:])
         make_identity(nc, ident_f32[:])
         b_row = keep.tile([P, D], BF16, name="b_row")
-        nc.gpsimd.memset(b_row[:], 0.0)
-        ones = keep.tile([P, P], BF16, name="ones")
-        nc.gpsimd.memset(ones[:], 1.0)
+        ones = keep.tile([P, D_HALF], BF16, name="ones")
+        nc.vector.memset(ones[:], 1.0)
+        nc.vector.memset(b_row[:], 0.0)
 
         tiles = {}
 
@@ -147,10 +147,14 @@ def tile_gau_pa_kernel(tc, q, k, v, gate, W_out, b_out, x, out):
             dst = kT if what == "k" else qT
             copy(out=dst[:, 4 * half : 4 * half + 4, :], in_=tiles[("T" + what, half)][:])
 
+        def warm_up(n):
+            bank = psum_tile(psum_s, ("wu", n), [P, D_HALF], F32)
+            nc.tensor.matmul(out=bank[:], lhsT=ones[:, :P], rhs=ones[:], start=True, stop=True)
+
         def spread_bias(half):
             bank = psum_tile(psum_s, ("bb", half), [P, D_HALF], F32)
             cols = slice(D_HALF * half, D_HALF * (half + 1))
-            nc.tensor.matmul(out=bank[:], lhsT=ones[:], rhs=b_row[:, cols], start=True, stop=True)
+            nc.tensor.matmul(out=bank[:], lhsT=ones[:, :P], rhs=b_row[:, cols], start=True, stop=True)
 
         def keep_bias(half):
             cols = slice(D_HALF * half, D_HALF * (half + 1))
@@ -350,6 +354,8 @@ def tile_gau_pa_kernel(tc, q, k, v, gate, W_out, b_out, x, out):
                 return [("ld",) + i], ("ps", 1, ("T",) + i), [], lambda: turn_qk(*i)
             if kind == "C":
                 return [("T",) + i], None, [("T",) + i], lambda: keep_qk(i[0], i[1], copy)
+            if kind == "wu":
+                return [], ("ps", 0, ("wu",) + i), [], lambda: warm_up(*i)
             if kind == "bb":
                 return [("ld", "b", 0)], ("ps", 1, ("bb",) + i), [], lambda: spread_bias(*i)
             if kind == "bk":

@@ -25,30 +25,30 @@ D_HALF = 512
 
 FLOPS = 2 * S * S * QK + 2 * S * S * H + 2 * S * H * D
 
-LOADS = """ld.k.0 ld.q.0 ld.v.0.0 ld.k.1 ld.v.0.1 ld.q.1 ld.v.1.0 ld.v.1.1 ld.b.0 ld.v.2.0 ld.v.2.1 ld.g.0 ld.g.1
+LOADS = """ld.b.0 ld.k.0 ld.q.0 ld.v.0.0 ld.k.1 ld.v.0.1 ld.q.1 ld.v.1.0 ld.v.1.1 ld.v.2.0 ld.v.2.1 ld.g.0 ld.g.1
 ld.v.3.0 ld.v.3.1 ld.g.2 ld.W.0 ld.W.1 ld.g.3 ld.W.2 ld.W.3 ld.g.4 ld.g.5 ld.g.6 ld.g.7"""
-TENSOR = """T.k.0 T.q.0 T.k.1 sc.0.0 sc.0.1 sc.1.0 sc.1.1 sc.2.0 sc.2.1 av.0.0 sc.3.0 sc.3.1 av.1.0 T.q.1 sc.4.0 sc.4.1
-av.2.0 av.0.1 av.1.1 bb.0 bb.1 sc.5.0 sc.5.1 av.2.1 vt.0.0 vt.1.0 wt.0.0 av.0.2 av.1.2 av.2.2 vt.2.0 wt.1.0
-wt.2.0 wt.3.0 av.0.3 wt.0.1 wt.1.1 av.1.3 av.2.3 av.3.0 av.3.1 vt.0.1 vt.1.1 wt.2.1 wt.3.1 av.3.2 av.3.3
-vt.2.1 wt.0.2 wt.1.2 sc.6.0 sc.6.1 av.4.0 av.4.1 vt.3.0 vt.3.1 wt.2.2 wt.3.2 wt.0.3 av.4.2 av.4.3 av.5.0
-av.5.1 wt.1.3 wt.2.3 wt.3.3 av.5.2 vt.4.0 vt.4.1 sc.7.0 sc.7.1 av.5.3 pj.0.0 pj.0.1 av.6.0 av.6.1 vt.5.0
-vt.5.1 pj.1.0 pj.1.1 av.6.2 av.6.3 pj.2.0 pj.2.1 vt.6.0 vt.6.1 av.7.0 av.7.1 pj.3.0 pj.3.1 av.7.2 av.7.3
-pj.4.0 pj.4.1 vt.7.0 vt.7.1 pj.5.0 pj.5.1 pj.6.0 pj.6.1 pj.7.0 pq.7.2 pq.7.3"""
-SCALAR = """C.k.1 re.0.0 re.0.1 re.1.0 sq.0 re.1.1 re.2.0 sq.1 re.2.1 re.3.0 sq.2 C.q.1 re.3.1 re.4.0 sq.3 re.4.1 bk.0
-bk.1 re.5.0 sq.4 re.5.1 sq.5 ve.0.0 ve.1.0 we.0.0 ve.2.0 we.1.0 we.2.0 we.3.0 we.0.1 we.1.1 ve.0.1 ve.1.1
-we.2.1 we.3.1 ve.2.1 we.0.2 we.1.2 re.6.0 re.6.1 ve.3.0 ve.3.1 sq.6 ld.x.0 we.2.2 we.3.2 we.0.3 we.1.3 we.2.3
-we.3.3 ve.4.0 ve.4.1 re.7.0 re.7.1 ld.x.1 sq.7 ve.5.0 ve.5.1 ve.6.0 ve.6.1 ve.7.0 ve.7.1"""
-VECTOR = """C.k.0 C.q.0 vc.0.0.0 vc.0.0.1 vc.0.1.0 vc.0.1.1 qv.0.0 qv.0.1 vc.1.0.0 qA.0 vc.1.0.1 vc.1.1.0 vc.1.1.1 qv.1.0
-qA.1 qv.1.1 vc.2.0.0 vc.2.0.1 ga.0.0 qA.2 vc.2.1.0 vc.2.1.1 ga.1.0 qv.2.0 ga.0.1 qv.2.1 ga.2.0 vc.3.0.0
-vc.3.0.1 ga.1.1 vc.3.1.0 vc.3.1.1 ga.2.1 qA.3 qv.3.0 qV.0.0 qv.3.1 qV.1.0 ga.0.2 qA.4 ga.1.2 qV.2.0 ga.2.2
+TENSOR = """T.k.0 T.q.0 bb.0 bb.1 T.k.1 sc.0.0 sc.0.1 sc.1.0 sc.1.1 sc.2.0 sc.2.1 av.0.0 sc.3.0 sc.3.1 av.1.0 T.q.1
+sc.4.0 sc.4.1 av.2.0 av.0.1 av.1.1 sc.5.0 sc.5.1 av.2.1 vt.0.0 vt.1.0 av.0.2 wt.0.0 av.1.2 av.2.2 vt.2.0
+wt.1.0 wt.2.0 wt.3.0 av.0.3 wt.0.1 wt.1.1 av.1.3 av.2.3 sc.6.0 sc.6.1 av.3.0 av.3.1 vt.0.1 vt.1.1 wt.2.1
+wt.3.1 av.3.2 av.3.3 vt.2.1 wt.0.2 wt.1.2 av.4.0 av.4.1 av.4.2 vt.3.0 vt.3.1 wt.2.2 wt.3.2 av.4.3 av.5.0
+av.5.1 wt.0.3 wt.1.3 wt.2.3 av.5.2 wt.3.3 vt.4.0 vt.4.1 sc.7.0 sc.7.1 av.5.3 pj.0.0 pj.0.1 av.6.0 av.6.1
+vt.5.0 vt.5.1 pj.1.0 pj.1.1 av.6.2 av.6.3 pj.2.0 pj.2.1 vt.6.0 vt.6.1 av.7.0 av.7.1 pj.3.0 pj.3.1 av.7.2
+av.7.3 pj.4.0 pj.4.1 vt.7.0 vt.7.1 pj.5.0 pj.5.1 pj.6.0 pj.6.1 pj.7.0 pq.7.2 pq.7.3"""
+SCALAR = """bk.0 bk.1 C.k.1 re.0.0 re.0.1 re.1.0 sq.0 re.1.1 re.2.0 sq.1 re.2.1 re.3.0 sq.2 C.q.1 re.3.1 re.4.0 sq.3
+re.4.1 re.5.0 sq.4 re.5.1 sq.5 ve.0.0 ve.1.0 we.0.0 ve.2.0 we.1.0 we.2.0 we.3.0 we.0.1 we.1.1 re.6.0 re.6.1
+ve.0.1 ve.1.1 we.2.1 we.3.1 sq.6 ve.2.1 we.0.2 we.1.2 ve.3.0 ve.3.1 ld.x.0 we.2.2 we.3.2 we.0.3 we.1.3 we.2.3
+ld.x.1 we.3.3 ve.4.0 ve.4.1 re.7.0 re.7.1 ld.x.2 ld.x.3 sq.7 ve.5.0 ve.5.1 ve.6.0 ve.6.1 ve.7.0 ve.7.1"""
+VECTOR = """C.k.0 C.q.0 vc.0.0.0 vc.0.0.1 vc.0.1.0 vc.0.1.1 qv.0.0 qv.0.1 vc.1.0.0 vc.1.0.1 qA.0 vc.1.1.0 vc.1.1.1 qv.1.0
+qv.1.1 qA.1 vc.2.0.0 vc.2.0.1 ga.0.0 qA.2 vc.2.1.0 vc.2.1.1 ga.1.0 qv.2.0 ga.0.1 ga.1.1 qv.2.1 ga.2.0
+vc.3.0.0 vc.3.0.1 vc.3.1.0 vc.3.1.1 ga.2.1 qA.3 qv.3.0 qV.0.0 qv.3.1 qV.1.0 ga.0.2 qA.4 ga.1.2 qV.2.0 ga.2.2
 ga.0.3 ga.1.3 ga.2.3 ga.3.0 qA.5 ga.3.1 qW.0.0 qV.0.1 qW.1.0 qV.1.1 ga.3.2 qW.2.0 qV.2.1 ga.3.3 qW.3.0 ga.4.0
-ga.4.1 qV.3.0 qV.3.1 ga.4.2 ga.4.3 qA.6 ga.5.0 qW.0.1 qW.1.1 ga.5.1 qW.2.1 ga.5.2 qW.3.1 qV.4.0 qV.4.1 ga.5.3
-fi.0.0 fi.0.1 qA.7 ga.6.0 ga.6.1 qV.5.0 qV.5.1 fi.1.0 fi.1.1 ga.6.2 ga.6.3 rs.4 fi.2.0 fi.2.1 qV.6.0 qV.6.1
+ga.4.1 qV.3.0 qV.3.1 ga.4.2 ga.4.3 qA.6 ga.5.0 qW.0.1 qW.1.1 ga.5.1 qW.2.1 ga.5.2 qW.3.1 ga.5.3 fi.0.0 fi.0.1
+qA.7 ga.6.0 ga.6.1 qV.4.0 qV.4.1 fi.1.0 fi.1.1 qV.5.0 qV.5.1 ga.6.2 ga.6.3 rs.4 fi.2.0 fi.2.1 qV.6.0 qV.6.1
 ga.7.0 ga.7.1 fi.3.0 fi.3.1 rs.5 ga.7.2 ga.7.3 fi.4.0 fi.4.1 rs.6 qV.7.0 qV.7.1 fi.5.0 fi.5.1 rs.7 fi.6.0
 fi.6.1 fi.7.0 fq.7.2 fq.7.3"""
 GPSIMD = "rs.0 rs.1 rs.2 rs.3"
 
-RING_BUFS = {"raw":5,"gate":6,"relu":3,"a_grp":4,"grp":5,"gated":8,"v_t":4,"resid":4,"ps":4,"pv":4}
+RING_BUFS = {"raw":4,"gate":8,"relu":3,"a_grp":4,"grp":5,"gated":8,"v_t":4,"resid":4,"ps":4,"pv":4}
 
 
 def tile_gau_pa_kernel(tc, q, k, v, gate, W_out, b_out, x, out):
@@ -86,8 +86,8 @@ def tile_gau_pa_kernel(tc, q, k, v, gate, W_out, b_out, x, out):
         make_identity(nc, ident_f32[:])
         b_row = keep.tile([P, D], BF16, name="b_row")
         ones = keep.tile([P, D_HALF], BF16, name="ones")
-        nc.vector.memset(ones[:], 1.0)
         nc.vector.memset(b_row[:], 0.0)
+        nc.vector.memset(ones[:], 1.0)
 
         tiles = {}
 
@@ -111,7 +111,7 @@ def tile_gau_pa_kernel(tc, q, k, v, gate, W_out, b_out, x, out):
                     in_=q_rows.rearrange("(p a) d -> p a d", a=BLOCKS)[:, 4 * i : 4 * i + 4, :],
                 )
             elif what == "b":
-                nc.sync.dma_start(out=b_row[0:1, :], in_=b_out.rearrange("(o d) -> o d", o=1))
+                nc.scalar.dma_start(out=b_row[0:1, :], in_=b_out.rearrange("(o d) -> o d", o=1))
             elif what == "v":
                 if ("v", i) not in tiles:
                     ring_tile("raw", ("v", i), [P, KEY_PASSES * PACK * K_PASS], BF16)
@@ -121,6 +121,12 @@ def tile_gau_pa_kernel(tc, q, k, v, gate, W_out, b_out, x, out):
                     in_=v_rows[K_PASS * c : K_PASS * (c + 1), K_PASS * i : K_PASS * (i + 1)].rearrange(
                         "(p t) h -> p t h", t=PACK
                     ),
+                )
+            elif what == "w":
+                raw = ring_tile("raw", ("w", i), [P, PACK * 2 * K_PASS], BF16)
+                nc.sync.dma_start(
+                    out=raw[:].rearrange("p (t h) -> p t h", t=PACK),
+                    in_=v_rows[K_PASS * i : K_PASS * (i + 1), 2 * K_PASS :].rearrange("(p t) h -> p t h", t=PACK),
                 )
             elif what == "g":
                 raw = ring_tile("gate", ("g", i), [P, H], BF16)
@@ -132,9 +138,9 @@ def tile_gau_pa_kernel(tc, q, k, v, gate, W_out, b_out, x, out):
                     in_=W_out[2 * P * i : 2 * P * (i + 1), :].rearrange("(n p) h -> p n h", p=P),
                 )
             else:
-                raw = ring_tile("raw", ("x", i), [P, 4 * D], BF16)
+                raw = ring_tile("gate", ("x", i), [P, 2 * D], BF16)
                 queue.dma_start(
-                    out=raw[:].rearrange("p (a d) -> p a d", a=4), in_=x_rows[:, 4 * i : 4 * i + 4, :]
+                    out=raw[:].rearrange("p (a d) -> p a d", a=2), in_=x_rows[:, 2 * i : 2 * i + 2, :]
                 )
 
         def turn_qk(what, half):
@@ -191,10 +197,13 @@ def tile_gau_pa_kernel(tc, q, k, v, gate, W_out, b_out, x, out):
         def group_v(g, c, half, copy):
             if ("vg", g, c) not in tiles:
                 ring_tile("grp", ("vg", g, c), [P, K_PASS * PACK], BF16)
-            src = tiles[("v", g)][:].rearrange("p (c t n i) -> p c n t i", c=KEY_PASSES, t=PACK, i=4)
+            if ("w", c) in tiles and g >= 2:
+                src = tiles[("w", c)][:].rearrange("p (t e n i) -> p e n t i", t=PACK, e=2, i=4)[:, g - 2, :, :, :]
+            else:
+                src = tiles[("v", g)][:].rearrange("p (c t n i) -> p c n t i", c=KEY_PASSES, t=PACK, i=4)[:, c, :, :, :]
             dst = tiles[("vg", g, c)][:].rearrange("p (n i t) -> p n t i", i=4, t=PACK)
             rows = slice(64 * half, 64 * half + 64)
-            copy(out=dst[:, rows, :, :], in_=src[:, c, rows, :, :])
+            copy(out=dst[:, rows, :, :], in_=src[:, rows, :, :])
 
         def quantise_v(g, c):
             cols = slice(K_PASS * c, K_PASS * (c + 1))
@@ -276,9 +285,9 @@ def tile_gau_pa_kernel(tc, q, k, v, gate, W_out, b_out, x, out):
             res = ring_tile("resid", ("rs", a), [P, D], F32)
             for n in range(pieces):
                 cols = slice(D // pieces * n, D // pieces * (n + 1))
-                x_view = tiles[("x", a // 4)][:].rearrange("p (a d) -> p a d", a=4)
+                x_view = tiles[("x", a // 2)][:].rearrange("p (a d) -> p a d", a=2)
                 engine.tensor_tensor(
-                    out=res[:, cols], in0=x_view[:, a % 4, cols], in1=bias_all[:, cols], op=ALU.add
+                    out=res[:, cols], in0=x_view[:, a % 2, cols], in1=bias_all[:, cols], op=ALU.add
                 )
 
         def project(a, half):
@@ -331,9 +340,9 @@ def tile_gau_pa_kernel(tc, q, k, v, gate, W_out, b_out, x, out):
             d_cols = slice(D_HALF * half, D_HALF * (half + 1))
             if half == 0:
                 ring_tile("resid", ("rs", a), [P, D], F32)
-            x_view = tiles[("x", a // 4)][:].rearrange("p (a d) -> p a d", a=4)
+            x_view = tiles[("x", a // 2)][:].rearrange("p (a d) -> p a d", a=2)
             nc.vector.tensor_tensor(
-                out=tiles[("rs", a)][:, d_cols], in0=tiles[("pj", a, half)][:], in1=x_view[:, a % 4, d_cols], op=ALU.add
+                out=tiles[("rs", a)][:, d_cols], in0=tiles[("pj", a, half)][:], in1=x_view[:, a % 2, d_cols], op=ALU.add
             )
 
         def add_bias(a, half):
@@ -347,7 +356,7 @@ def tile_gau_pa_kernel(tc, q, k, v, gate, W_out, b_out, x, out):
             if kind == "ld":
                 what, n = i[:2]
                 c = i[2] if what == "v" else 0
-                buf = {"v": ("raw", 4), "W": ("raw", 4), "x": ("raw", 4), "g": ("gate", 4)}
+                buf = {"w": ("raw", 4), "v": ("raw", 4), "W": ("raw", 4), "x": ("gate", 2), "g": ("gate", 4)}
                 opens = buf[what] + (("ld", what, n),) if what in buf and ("ld", what, n) not in left else None
                 return [], opens, [], lambda: load(what, n, c, nc.scalar if engine == "S" else nc.sync)
             if kind == "T":
@@ -371,6 +380,8 @@ def tile_gau_pa_kernel(tc, q, k, v, gate, W_out, b_out, x, out):
                 return [("sq",) + i], None, [("sq",) + i], lambda: quantise_a(*i)
             if kind == "vc":
                 opens = ("grp", 1, ("vg",) + i[:2]) if ("vg",) + i[:2] not in left else None
+                if "ld.w.0" in LOADS and i[0] >= 2:
+                    return [("ld", "w", i[1])], opens, [("ld", "w", i[1])], lambda: group_v(i[0], i[1], i[2], copy)
                 return [("ld", "v", i[0], i[1])], opens, [("ld", "v", i[0])], lambda: group_v(i[0], i[1], i[2], copy)
             if kind == "qv":
                 return [("vc",) + i + (0,), ("vc",) + i + (1,)], None, [("vg",) + i], lambda: quantise_v(*i)
@@ -398,8 +409,8 @@ def tile_gau_pa_kernel(tc, q, k, v, gate, W_out, b_out, x, out):
             if kind == "rs":
                 a = i[0]
                 where = (nc.vector, 1) if engine == "V" else (nc.gpsimd, 4)
-                needs = [("ld", "x", a // 4), ("bk", 0), ("bk", 1)]
-                return needs, ("resid", 2, ("rs", a)), [("ld", "x", a // 4)], lambda: residual(a, *where)
+                needs = [("ld", "x", a // 2), ("bk", 0), ("bk", 1)]
+                return needs, ("resid", 2, ("rs", a)), [("ld", "x", a // 2)], lambda: residual(a, *where)
             if kind == "pj":
                 a, h = i
                 needs = [("qV", a, 0), ("qV", a, 1)] + [("qW", g, h) for g in range(HID_PASSES)]
@@ -412,7 +423,7 @@ def tile_gau_pa_kernel(tc, q, k, v, gate, W_out, b_out, x, out):
                 return [("pq",) + i, ("rs", i[0])], None, [("pq",) + i, ("rs", i[0])], lambda: finish_piece(*i)
             if kind == "fx":
                 opens = ("resid", 2, ("rs", i[0])) if i[1] == 0 else None
-                return [("pj",) + i, ("ld", "x", i[0] // 4)], opens, [("pj",) + i, ("ld", "x", i[0] // 4)], lambda: add_residual(*i)
+                return [("pj",) + i, ("ld", "x", i[0] // 2)], opens, [("pj",) + i, ("ld", "x", i[0] // 2)], lambda: add_residual(*i)
             if kind == "gb":
                 return [("fx",) + i, ("bk", 0), ("bk", 1)], None, [("rs", i[0])], lambda: add_bias(*i)
             return [("pj",) + i, ("rs", i[0])], None, [("pj",) + i, ("rs", i[0])], lambda: finish(*i)
@@ -425,7 +436,7 @@ def tile_gau_pa_kernel(tc, q, k, v, gate, W_out, b_out, x, out):
             lane = []
             for word in text.split():
                 parts = word.split(".")
-                lane.append((parts[0], tuple([n if n in ("k", "q", "v", "W", "g", "b", "x") else int(n) for n in parts[1:]])))
+                lane.append((parts[0], tuple([n if n in ("k", "q", "v", "w", "W", "g", "b", "x") else int(n) for n in parts[1:]])))
             lanes.append([engine, lane, 0])
         moved = True
         while moved:

@@ -25,22 +25,22 @@ D_HALF = 512
 
 FLOPS = 2 * S * S * QK + 2 * S * S * H + 2 * S * H * D
 
-LOADS = """ld.b.0 ld.k.0 ld.q.0 ld.v.0.0 ld.k.1 ld.v.0.1 ld.q.1 ld.v.1.0 ld.v.1.1 ld.v.2.0 ld.v.2.1 ld.g.0 ld.g.1
-ld.v.3.0 ld.v.3.1 ld.g.2 ld.W.0 ld.W.1 ld.g.3 ld.W.2 ld.W.3 ld.g.4 ld.g.5 ld.g.6 ld.g.7"""
-TENSOR = """T.k.0 T.q.0 bb.0 bb.1 T.k.1 sc.0.0 sc.0.1 sc.1.0 sc.1.1 sc.2.0 sc.2.1 av.0.0 sc.3.0 sc.3.1 av.1.0 T.q.1
-sc.4.0 sc.4.1 av.2.0 av.0.1 av.1.1 sc.5.0 sc.5.1 av.2.1 vt.0.0 vt.1.0 av.0.2 wt.0.0 av.1.2 av.2.2 vt.2.0
-wt.1.0 wt.2.0 wt.3.0 av.0.3 wt.0.1 wt.1.1 av.1.3 av.2.3 sc.6.0 sc.6.1 av.3.0 av.3.1 vt.0.1 vt.1.1 wt.2.1
-wt.3.1 av.3.2 av.3.3 vt.2.1 wt.0.2 wt.1.2 av.4.0 av.4.1 av.4.2 vt.3.0 vt.3.1 wt.2.2 wt.3.2 av.4.3 av.5.0
-av.5.1 wt.0.3 wt.1.3 wt.2.3 av.5.2 wt.3.3 vt.4.0 vt.4.1 sc.7.0 sc.7.1 av.5.3 pj.0.0 pj.0.1 av.6.0 av.6.1
-vt.5.0 vt.5.1 pj.1.0 pj.1.1 av.6.2 av.6.3 pj.2.0 pj.2.1 vt.6.0 vt.6.1 av.7.0 av.7.1 pj.3.0 pj.3.1 av.7.2
-av.7.3 pj.4.0 pj.4.1 vt.7.0 vt.7.1 pj.5.0 pj.5.1 pj.6.0 pj.6.1 pj.7.0 pq.7.2 pq.7.3"""
-SCALAR = """bk.0 bk.1 C.k.1 re.0.0 re.0.1 re.1.0 sq.0 re.1.1 re.2.0 sq.1 re.2.1 re.3.0 sq.2 C.q.1 re.3.1 re.4.0 sq.3
-re.4.1 re.5.0 sq.4 re.5.1 sq.5 ve.0.0 ve.1.0 we.0.0 ve.2.0 we.1.0 we.2.0 we.3.0 we.0.1 we.1.1 re.6.0 re.6.1
+LOADS = """ld.k.0 ld.q.0 ld.k.1 ld.v.0.0 ld.v.0.1 ld.q.1 ld.v.1.0 ld.v.1.1 ld.b.0 ld.v.2.0 ld.v.2.1 ld.g.0 ld.g.1
+ld.v.3.0 ld.W.0 ld.v.3.1 ld.g.2 ld.W.1 ld.g.3 ld.W.2 ld.W.3 ld.g.4 ld.g.5 ld.g.6 ld.g.7"""
+TENSOR = """T.k.0 T.q.0 T.k.1 sc.0.0 sc.0.1 sc.1.0 sc.1.1 sc.2.0 sc.2.1 av.0.0 sc.3.0 sc.3.1 av.1.0 T.q.1 sc.4.0 sc.4.1
+av.0.1 av.1.1 bb.0 bb.1 av.2.0 av.2.1 vt.0.0 vt.1.0 wt.0.0 wt.1.0 av.0.2 av.1.2 wt.2.0 wt.3.0 av.2.2 sc.5.0
+sc.5.1 vt.2.0 av.0.3 wt.0.1 wt.1.1 av.1.3 av.2.3 sc.6.0 sc.6.1 av.3.0 av.3.1 vt.0.1 vt.1.1 wt.2.1 wt.3.1
+av.3.2 av.3.3 vt.2.1 wt.0.2 wt.1.2 av.4.0 av.4.1 av.4.2 vt.3.0 vt.3.1 wt.2.2 wt.3.2 av.4.3 av.5.0 av.5.1
+wt.0.3 wt.1.3 wt.2.3 av.5.2 wt.3.3 vt.4.0 vt.4.1 sc.7.0 sc.7.1 av.5.3 pj.0.0 pj.0.1 av.6.0 av.6.1 vt.5.0
+vt.5.1 pj.1.0 pj.1.1 av.6.2 av.6.3 pj.2.0 pj.2.1 vt.6.0 vt.6.1 av.7.0 av.7.1 pj.3.0 pj.3.1 av.7.2 av.7.3
+pj.4.0 pj.4.1 vt.7.0 vt.7.1 pj.5.0 pj.5.1 pj.6.0 pj.6.1 pj.7.0 pq.7.2 pq.7.3"""
+SCALAR = """C.k.1 re.0.0 re.0.1 re.1.0 sq.0 re.1.1 re.2.0 sq.1 re.2.1 re.3.0 sq.2 C.q.1 re.3.1 re.4.0 sq.3 re.4.1 bk.0
+bk.1 sq.4 ve.0.0 ve.1.0 we.0.0 we.1.0 we.2.0 we.3.0 re.5.0 re.5.1 ve.2.0 sq.5 we.0.1 we.1.1 re.6.0 re.6.1
 ve.0.1 ve.1.1 we.2.1 we.3.1 sq.6 ve.2.1 we.0.2 we.1.2 ve.3.0 ve.3.1 ld.x.0 we.2.2 we.3.2 we.0.3 we.1.3 we.2.3
 ld.x.1 we.3.3 ve.4.0 ve.4.1 re.7.0 re.7.1 ld.x.2 ld.x.3 sq.7 ve.5.0 ve.5.1 ve.6.0 ve.6.1 ve.7.0 ve.7.1"""
 VECTOR = """C.k.0 C.q.0 vc.0.0.0 vc.0.0.1 vc.0.1.0 vc.0.1.1 qv.0.0 qv.0.1 vc.1.0.0 vc.1.0.1 qA.0 vc.1.1.0 vc.1.1.1 qv.1.0
-qv.1.1 qA.1 vc.2.0.0 vc.2.0.1 ga.0.0 qA.2 vc.2.1.0 vc.2.1.1 ga.1.0 qv.2.0 ga.0.1 ga.1.1 qv.2.1 ga.2.0
-vc.3.0.0 vc.3.0.1 vc.3.1.0 vc.3.1.1 ga.2.1 qA.3 qv.3.0 qV.0.0 qv.3.1 qV.1.0 ga.0.2 qA.4 ga.1.2 qV.2.0 ga.2.2
+qv.1.1 qA.1 vc.2.0.0 vc.2.0.1 ga.0.0 qA.2 vc.2.1.0 vc.2.1.1 ga.1.0 qv.2.0 ga.0.1 ga.1.1 qv.2.1 vc.3.0.0
+vc.3.0.1 vc.3.1.0 vc.3.1.1 ga.2.0 ga.2.1 qv.3.0 qv.3.1 qA.3 qV.0.0 qV.1.0 ga.0.2 qA.4 ga.1.2 qV.2.0 ga.2.2
 ga.0.3 ga.1.3 ga.2.3 ga.3.0 qA.5 ga.3.1 qW.0.0 qV.0.1 qW.1.0 qV.1.1 ga.3.2 qW.2.0 qV.2.1 ga.3.3 qW.3.0 ga.4.0
 ga.4.1 qV.3.0 qV.3.1 ga.4.2 ga.4.3 qA.6 ga.5.0 qW.0.1 qW.1.1 ga.5.1 qW.2.1 ga.5.2 qW.3.1 ga.5.3 fi.0.0 fi.0.1
 qA.7 ga.6.0 ga.6.1 qV.4.0 qV.4.1 fi.1.0 fi.1.1 qV.5.0 qV.5.1 ga.6.2 ga.6.3 rs.4 fi.2.0 fi.2.1 qV.6.0 qV.6.1
@@ -111,7 +111,7 @@ def tile_gau_pa_kernel(tc, q, k, v, gate, W_out, b_out, x, out):
                     in_=q_rows.rearrange("(p a) d -> p a d", a=BLOCKS)[:, 4 * i : 4 * i + 4, :],
                 )
             elif what == "b":
-                nc.scalar.dma_start(out=b_row[0:1, :], in_=b_out.rearrange("(o d) -> o d", o=1))
+                nc.sync.dma_start(out=b_row[0:1, :], in_=b_out.rearrange("(o d) -> o d", o=1))
             elif what == "v":
                 if ("v", i) not in tiles:
                     ring_tile("raw", ("v", i), [P, KEY_PASSES * PACK * K_PASS], BF16)

@@ -27,25 +27,26 @@ FLOPS = 2 * S * S * QK + 2 * S * S * H + 2 * S * H * D
 
 LOADS = """ld.k.0 ld.q.0 ld.k.1 ld.v.0.0 ld.v.0.1 ld.q.1 ld.v.1.0 ld.v.1.1 ld.b.0 ld.v.2.0 ld.v.2.1 ld.g.0 ld.g.1
 ld.v.3.0 ld.W.0 ld.v.3.1 ld.g.2 ld.W.1 ld.g.3 ld.W.2 ld.W.3 ld.g.4 ld.g.5 ld.g.6 ld.g.7"""
-TENSOR = """T.k.0 T.q.0 T.k.1 sc.0.0 sc.0.1 sc.1.0 sc.1.1 sc.2.0 sc.2.1 av.0.0 sc.3.0 sc.3.1 av.1.0 T.q.1 sc.4.0 sc.4.1
+TENSOR = """T.k.0 T.q.0 T.k.1 sc.0.0 sc.0.1 sc.1.0 sc.1.1 sc.2.0 sc.2.1 T.q.1 sc.3.0 sc.3.1 av.0.0 sc.4.0 sc.4.1 av.1.0
 av.0.1 av.1.1 bb.0 bb.1 av.2.0 av.2.1 vt.0.0 vt.1.0 wt.0.0 wt.1.0 av.0.2 av.1.2 wt.2.0 wt.3.0 av.2.2 sc.5.0
-sc.5.1 vt.2.0 av.0.3 wt.0.1 wt.1.1 av.1.3 av.2.3 sc.6.0 sc.6.1 av.3.0 av.3.1 vt.0.1 vt.1.1 wt.2.1 wt.3.1
+sc.5.1 av.0.3 vt.2.0 wt.0.1 wt.1.1 av.1.3 av.2.3 sc.6.0 sc.6.1 av.3.0 av.3.1 vt.0.1 vt.1.1 wt.2.1 wt.3.1
 av.3.2 av.3.3 vt.2.1 wt.0.2 wt.1.2 av.4.0 av.4.1 av.4.2 vt.3.0 vt.3.1 wt.2.2 wt.3.2 av.4.3 av.5.0 av.5.1
 wt.0.3 wt.1.3 wt.2.3 av.5.2 wt.3.3 vt.4.0 vt.4.1 sc.7.0 sc.7.1 av.5.3 pj.0.0 pj.0.1 av.6.0 av.6.1 vt.5.0
 vt.5.1 pj.1.0 pj.1.1 av.6.2 av.6.3 pj.2.0 pj.2.1 vt.6.0 vt.6.1 av.7.0 av.7.1 pj.3.0 pj.3.1 av.7.2 av.7.3
 pj.4.0 pj.4.1 vt.7.0 vt.7.1 pj.5.0 pj.5.1 pj.6.0 pj.6.1 pj.7.0 pq.7.2 pq.7.3"""
-SCALAR = """C.k.1 re.0.0 re.0.1 re.1.0 sq.0 re.1.1 re.2.0 sq.1 re.2.1 re.3.0 sq.2 C.q.1 re.3.1 re.4.0 sq.3 re.4.1 bk.0
-bk.1 sq.4 ve.0.0 ve.1.0 we.0.0 we.1.0 we.2.0 we.3.0 re.5.0 re.5.1 ve.2.0 sq.5 we.0.1 we.1.1 re.6.0 re.6.1
-ve.0.1 ve.1.1 we.2.1 we.3.1 sq.6 ve.2.1 we.0.2 we.1.2 ve.3.0 ve.3.1 ld.x.0 we.2.2 we.3.2 we.0.3 we.1.3 we.2.3
-ld.x.1 we.3.3 ve.4.0 ve.4.1 re.7.0 re.7.1 ld.x.2 ld.x.3 sq.7 ve.5.0 ve.5.1 ve.6.0 ve.6.1 ve.7.0 ve.7.1"""
+SCALAR = """C.k.1 re.0.0 re.0.1 re.1.0 sq.0 re.1.1 re.2.0 sq.1 re.2.1 C.q.1 re.3.0 sq.2 re.3.1 vc.2.1.1 re.4.0 sq.3
+re.4.1 bk.0 bk.1 sq.4 ve.0.0 ve.1.0 vc.3.1.1 we.0.0 we.1.0 we.2.0 we.3.0 re.5.0 re.5.1 ve.2.0 sq.5 we.0.1
+we.1.1 re.6.0 re.6.1 ve.0.1 ve.1.1 we.2.1 we.3.1 sq.6 ve.2.1 we.0.2 we.1.2 ve.3.0 ve.3.1 ld.x.0 we.2.2 we.3.2
+we.0.3 we.1.3 we.2.3 ld.x.1 we.3.3 ve.4.0 ve.4.1 re.7.0 re.7.1 ld.x.2 ld.x.3 sq.7 ve.5.0 ve.5.1 ve.6.0 ve.6.1
+ve.7.0 ve.7.1"""
 VECTOR = """C.k.0 C.q.0 vc.0.0.0 vc.0.0.1 vc.0.1.0 vc.0.1.1 qv.0.0 qv.0.1 vc.1.0.0 vc.1.0.1 qA.0 vc.1.1.0 vc.1.1.1 qv.1.0
-qv.1.1 qA.1 vc.2.0.0 vc.2.0.1 ga.0.0 qA.2 vc.2.1.0 vc.2.1.1 ga.1.0 qv.2.0 ga.0.1 ga.1.1 qv.2.1 vc.3.0.0
-vc.3.0.1 vc.3.1.0 vc.3.1.1 ga.2.0 ga.2.1 qv.3.0 qv.3.1 qA.3 qV.0.0 qV.1.0 ga.0.2 qA.4 ga.1.2 qV.2.0 ga.2.2
-ga.0.3 ga.1.3 ga.2.3 ga.3.0 qA.5 ga.3.1 qW.0.0 qV.0.1 qW.1.0 qV.1.1 ga.3.2 qW.2.0 qV.2.1 ga.3.3 qW.3.0 ga.4.0
-ga.4.1 qV.3.0 qV.3.1 ga.4.2 ga.4.3 qA.6 ga.5.0 qW.0.1 qW.1.1 ga.5.1 qW.2.1 ga.5.2 qW.3.1 ga.5.3 fi.0.0 fi.0.1
-qA.7 ga.6.0 ga.6.1 qV.4.0 qV.4.1 fi.1.0 fi.1.1 qV.5.0 qV.5.1 ga.6.2 ga.6.3 rs.4 fi.2.0 fi.2.1 qV.6.0 qV.6.1
-ga.7.0 ga.7.1 fi.3.0 fi.3.1 rs.5 ga.7.2 ga.7.3 fi.4.0 fi.4.1 rs.6 qV.7.0 qV.7.1 fi.5.0 fi.5.1 rs.7 fi.6.0
-fi.6.1 fi.7.0 fq.7.2 fq.7.3"""
+qv.1.1 qA.1 vc.2.0.0 vc.2.0.1 ga.0.0 qA.2 vc.2.1.0 ga.1.0 qv.2.0 ga.0.1 ga.1.1 qv.2.1 vc.3.0.0 vc.3.0.1
+vc.3.1.0 ga.2.0 ga.2.1 qv.3.0 qv.3.1 qA.3 qV.0.0 qV.1.0 ga.0.2 qA.4 ga.1.2 qV.2.0 ga.2.2 ga.0.3 ga.1.3 ga.2.3
+ga.3.0 qA.5 ga.3.1 qW.0.0 qV.0.1 qW.1.0 qV.1.1 ga.3.2 qW.2.0 qV.2.1 ga.3.3 qW.3.0 ga.4.0 ga.4.1 qV.3.0 qV.3.1
+ga.4.2 ga.4.3 qA.6 ga.5.0 qW.0.1 qW.1.1 ga.5.1 qW.2.1 ga.5.2 qW.3.1 ga.5.3 fi.0.0 fi.0.1 qA.7 ga.6.0 ga.6.1
+qV.4.0 qV.4.1 fi.1.0 fi.1.1 qV.5.0 qV.5.1 ga.6.2 ga.6.3 rs.4 fi.2.0 fi.2.1 qV.6.0 qV.6.1 ga.7.0 ga.7.1 fi.3.0
+fi.3.1 rs.5 ga.7.2 ga.7.3 fi.4.0 fi.4.1 rs.6 qV.7.0 qV.7.1 fi.5.0 fi.5.1 rs.7 fi.6.0 fi.6.1 fi.7.0 fq.7.2
+fq.7.3"""
 GPSIMD = "rs.0 rs.1 rs.2 rs.3"
 
 RING_BUFS = {"raw":4,"gate":8,"relu":3,"a_grp":4,"grp":5,"gated":8,"v_t":4,"resid":4,"ps":4,"pv":4}

@@ -36,7 +36,7 @@ vt.5.1 pj.1.0 pj.1.1 av.6.2 av.6.3 pj.2.0 pj.2.1 vt.6.0 vt.6.1 av.7.0 av.7.1 pj.
 pj.4.0 pj.4.1 vt.7.0 vt.7.1 pj.5.0 pj.5.1 pj.6.0 pj.6.1 pj.7.0 pq.7.2 pq.7.3"""
 SCALAR = """C.k.1 re.0.0 re.0.1 re.1.0 sq.0 re.1.1 re.2.0 sq.1 re.2.1 C.q.1 re.3.0 sq.2 re.3.1 vc.2.1.1 re.4.0 sq.3
 re.4.1 bk.0 bk.1 sq.4 ve.0.0 ve.1.0 vc.3.1.1 we.0.0 we.1.0 we.2.0 we.3.0 re.5.0 re.5.1 ve.2.0 sq.5 we.0.1
-we.1.1 re.6.0 re.6.1 ve.0.1 ve.1.1 we.2.1 we.3.1 sq.6 ve.2.1 we.0.2 we.1.2 ve.3.0 ve.3.1 ld.x.0 we.2.2 we.3.2
+we.1.1 re.6.0 re.6.1 ve.0.1 ve.1.1 we.2.1 we.3.1 ve.2.1 sq.6 we.0.2 we.1.2 ve.3.0 ve.3.1 ld.x.0 we.2.2 we.3.2
 we.0.3 we.1.3 we.2.3 ld.x.1 we.3.3 ve.4.0 ve.4.1 re.7.0 re.7.1 ld.x.2 ld.x.3 sq.7 ve.5.0 ve.5.1 ve.6.0 ve.6.1
 ve.7.0 ve.7.1"""
 VECTOR = """C.k.0 C.q.0 vc.0.0.0 vc.0.0.1 vc.0.1.0 vc.0.1.1 qv.0.0 qv.0.1 vc.1.0.0 vc.1.0.1 qA.0 vc.1.1.0 vc.1.1.1 qv.1.0
@@ -49,7 +49,7 @@ fi.3.1 rs.5 ga.7.2 ga.7.3 fi.4.0 fi.4.1 rs.6 qV.7.0 qV.7.1 fi.5.0 fi.5.1 rs.7 fi
 fq.7.3"""
 GPSIMD = "rs.0 rs.1 rs.2 rs.3"
 
-RING_BUFS = {"raw":4,"gate":8,"relu":3,"a_grp":4,"grp":5,"gated":8,"v_t":4,"resid":4,"ps":4,"pv":4}
+RING_BUFS = {"raw":4,"gate":8,"relu":2,"a_grp":3,"grp":5,"gated":6,"v_t":4,"resid":4,"ps":4,"pv":4}
 
 
 def tile_gau_pa_kernel(tc, q, k, v, gate, W_out, b_out, x, out):
@@ -86,7 +86,7 @@ def tile_gau_pa_kernel(tc, q, k, v, gate, W_out, b_out, x, out):
         make_identity(nc, ident_bf[:])
         make_identity(nc, ident_f32[:])
         b_row = keep.tile([P, D], BF16, name="b_row")
-        ones = keep.tile([P, D_HALF], BF16, name="ones")
+        ones = keep.tile([P, P], BF16, name="ones")
         nc.vector.memset(b_row[:], 0.0)
         nc.vector.memset(ones[:], 1.0)
 
@@ -156,12 +156,12 @@ def tile_gau_pa_kernel(tc, q, k, v, gate, W_out, b_out, x, out):
 
         def warm_up(n):
             bank = psum_tile(psum_s, ("wu", n), [P, D_HALF], F32)
-            nc.tensor.matmul(out=bank[:], lhsT=ones[:, :P], rhs=ones[:], start=True, stop=True)
+            nc.tensor.matmul(out=bank[:], lhsT=ones[:], rhs=b_row[:, :D_HALF], start=True, stop=True)
 
         def spread_bias(half):
             bank = psum_tile(psum_s, ("bb", half), [P, D_HALF], F32)
             cols = slice(D_HALF * half, D_HALF * (half + 1))
-            nc.tensor.matmul(out=bank[:], lhsT=ones[:, :P], rhs=b_row[:, cols], start=True, stop=True)
+            nc.tensor.matmul(out=bank[:], lhsT=ones[:], rhs=b_row[:, cols], start=True, stop=True)
 
         def keep_bias(half):
             cols = slice(D_HALF * half, D_HALF * (half + 1))
@@ -204,7 +204,12 @@ def tile_gau_pa_kernel(tc, q, k, v, gate, W_out, b_out, x, out):
                 src = tiles[("v", g)][:].rearrange("p (c t n i) -> p c n t i", c=KEY_PASSES, t=PACK, i=4)[:, c, :, :, :]
             dst = tiles[("vg", g, c)][:].rearrange("p (n i t) -> p n t i", i=4, t=PACK)
             rows = slice(64 * half, 64 * half + 64)
-            copy(out=dst[:, rows, :, :], in_=src[:, rows, :, :])
+            if copy == nc.scalar.copy:
+                hop = tiles[("v", g)][:].rearrange("p (c t h) -> p c h t", c=KEY_PASSES, t=PACK)[:, c, :, :]
+                cols = slice(256 * half, 256 * half + 256)
+                copy(out=tiles[("vg", g, c)][:].rearrange("p (h t) -> p h t", t=PACK)[:, cols, :], in_=hop[:, cols, :])
+            else:
+                copy(out=dst[:, rows, :, :], in_=src[:, rows, :, :])
 
         def quantise_v(g, c):
             cols = slice(K_PASS * c, K_PASS * (c + 1))

from contextlib import ExitStack

import concourse.mybir as mybir
from concourse.masks import make_identity

BF16 = mybir.dt.bfloat16
F32 = mybir.dt.float32
U32 = mybir.dt.uint32
U8 = mybir.dt.uint8
FP8X4 = mybir.dt.float8_e4m3fn_x4
ACT = mybir.ActivationFunctionType
ALU = mybir.AluOpType

P = 128
PACK = 4
K_PASS = P * PACK
S = 1024
QK = 128
H = 2048
D = 1024
BLOCKS = S // P
KEY_PASSES = S // K_PASS
HID_PASSES = H // K_PASS
D_HALF = 512

FLOPS = 2 * S * S * QK + 2 * S * S * H + 2 * S * H * D

LOADS = """ld.k.0 ld.q.0 ld.k.1 ld.v.0.0 ld.v.0.1 ld.q.1 ld.v.1.0 ld.v.1.1 ld.b.0 ld.v.2.0 ld.v.2.1 ld.g.0 ld.g.1
ld.v.3.0 ld.W.0 ld.v.3.1 ld.g.2 ld.W.1 ld.g.3 ld.W.2 ld.W.3 ld.g.4 ld.g.5 ld.g.6 ld.g.7"""
TENSOR = """T.k.0 T.q.0 T.k.1 sc.0.0 sc.0.1 sc.1.0 sc.1.1 sc.2.0 sc.2.1 T.q.1 sc.3.0 sc.3.1 av.0.0 sc.4.0 sc.4.1 av.1.0
av.0.1 av.1.1 bb.0 bb.1 av.2.0 av.2.1 vt.0.0 vt.1.0 wt.0.0 wt.1.0 av.0.2 av.1.2 wt.2.0 wt.3.0 av.2.2 sc.5.0
sc.5.1 av.0.3 vt.2.0 wt.0.1 wt.1.1 av.1.3 av.2.3 sc.6.0 sc.6.1 av.3.0 av.3.1 vt.0.1 vt.1.1 wt.2.1 wt.3.1
av.3.2 av.3.3 vt.2.1 wt.0.2 wt.1.2 av.4.0 av.4.1 av.4.2 vt.3.0 vt.3.1 wt.2.2 wt.3.2 av.4.3 av.5.0 av.5.1
wt.0.3 wt.1.3 wt.2.3 av.5.2 wt.3.3 vt.4.0 vt.4.1 sc.7.0 sc.7.1 av.5.3 pj.0.0 pj.0.1 av.6.0 av.6.1 vt.5.0
vt.5.1 pj.1.0 pj.1.1 av.6.2 av.6.3 pj.2.0 pj.2.1 vt.6.0 vt.6.1 av.7.0 av.7.1 pj.3.0 pj.3.1 av.7.2 av.7.3
pj.4.0 pj.4.1 vt.7.0 vt.7.1 pj.5.0 pj.5.1 pj.6.0 pj.6.1 pj.7.0 pq.7.2 pq.7.3"""
SCALAR = """C.k.1 re.0.0 re.0.1 re.1.0 sq.0 re.1.1 re.2.0 sq.1 re.2.1 C.q.1 re.3.0 sq.2 re.3.1 vc.2.1.1 re.4.0 sq.3
re.4.1 bk.0 bk.1 sq.4 ve.0.0 ve.1.0 vc.3.1.1 we.0.0 we.1.0 we.2.0 we.3.0 re.5.0 re.5.1 ve.2.0 sq.5 we.0.1
we.1.1 re.6.0 re.6.1 ve.0.1 ve.1.1 we.2.1 we.3.1 ve.2.1 sq.6 we.0.2 we.1.2 ve.3.0 ve.3.1 ld.x.0 we.2.2 we.3.2
we.0.3 we.1.3 we.2.3 ld.x.1 we.3.3 ve.4.0 ve.4.1 re.7.0 re.7.1 ld.x.2 ld.x.3 sq.7 ve.5.0 ve.5.1 ve.6.0 ve.6.1
ve.7.0 ve.7.1"""
VECTOR = """C.k.0 C.q.0 vc.0.0.0 vc.0.0.1 vc.0.1.0 vc.0.1.1 qv.0.0 qv.0.1 vc.1.0.0 vc.1.0.1 qA.0 vc.1.1.0 vc.1.1.1 qv.1.0
qv.1.1 qA.1 vc.2.0.0 vc.2.0.1 ga.0.0 qA.2 vc.2.1.0 ga.1.0 qv.2.0 ga.0.1 ga.1.1 qv.2.1 vc.3.0.0 vc.3.0.1
vc.3.1.0 ga.2.0 ga.2.1 qv.3.0 qv.3.1 qA.3 qV.0.0 qV.1.0 ga.0.2 qA.4 ga.1.2 qV.2.0 ga.2.2 ga.0.3 ga.1.3 ga.2.3
ga.3.0 qA.5 ga.3.1 qW.0.0 qV.0.1 qW.1.0 qV.1.1 ga.3.2 qW.2.0 qV.2.1 ga.3.3 qW.3.0 ga.4.0 ga.4.1 qV.3.0 qV.3.1
ga.4.2 ga.4.3 qA.6 ga.5.0 qW.0.1 qW.1.1 ga.5.1 qW.2.1 ga.5.2 qW.3.1 ga.5.3 fi.0.0 fi.0.1 qA.7 ga.6.0 ga.6.1
qV.4.0 qV.4.1 fi.1.0 fi.1.1 qV.5.0 qV.5.1 ga.6.2 ga.6.3 rs.4 fi.2.0 fi.2.1 qV.6.0 qV.6.1 ga.7.0 ga.7.1 fi.3.0
fi.3.1 rs.5 ga.7.2 ga.7.3 fi.4.0 fi.4.1 rs.6 qV.7.0 qV.7.1 fi.5.0 fi.5.1 rs.7 fi.6.0 fi.6.1 fi.7.0 fq.7.2
fq.7.3"""
GPSIMD = "rs.0 rs.1 rs.2 rs.3"

RING_BUFS = {"raw":4,"gate":8,"relu":2,"a_grp":3,"grp":5,"gated":6,"v_t":4,"resid":4,"ps":4,"pv":4}


def tile_gau_pa_kernel(tc, q, k, v, gate, W_out, b_out, x, out):
    nc = tc.nc
    q_rows = q.flatten_outer_dims()
    k_rows = k.flatten_outer_dims()
    v_rows = v.flatten_outer_dims()
    gate_rows = gate.flatten_outer_dims().rearrange("(p a) h -> p a h", a=BLOCKS)
    x_rows = x.flatten_outer_dims().rearrange("(p a) d -> p a d", a=BLOCKS)
    out_rows = out.flatten_outer_dims().rearrange("(p a) d -> p a d", a=BLOCKS)

    with ExitStack() as ctx:
        keep = ctx.enter_context(tc.tile_pool(name="keep", bufs=1))
        sbuf = ctx.enter_context(tc.tile_pool(name="sbuf", bufs=1))
        psum_s = ctx.enter_context(tc.psum_pool(name="psum_s", bufs=RING_BUFS["ps"]))
        psum_v = ctx.enter_context(tc.psum_pool(name="psum_v", bufs=RING_BUFS["pv"]))
        ctx.enter_context(tc.manual_schedule())

        k_sb = keep.tile([P, KEY_PASSES * PACK, QK], BF16, name="k_sb")
        q_sb = keep.tile([P, BLOCKS, QK], BF16, name="q_sb")
        bias_all = keep.tile([P, D], BF16, name="bias_all")
        ident_bf = keep.tile([P, P], BF16, name="ident_bf")
        ident_f32 = keep.tile([P, P], F32, name="ident_f32")
        kT = keep.tile([P, KEY_PASSES * PACK, P], BF16, name="kT")
        qT = keep.tile([P, BLOCKS, P], BF16, name="qT")
        a_codes = keep.tile([P, BLOCKS, KEY_PASSES * P], U32, name="a_codes", align_bytes=64)
        a_scales = keep.tile([P, BLOCKS, KEY_PASSES * P], U8, name="a_scales", align_bytes=64)
        v_codes = keep.tile([P, HID_PASSES, KEY_PASSES * K_PASS], U32, name="v_codes", align_bytes=64)
        v_scales = keep.tile([P, HID_PASSES, KEY_PASSES * K_PASS], U8, name="v_scales", align_bytes=64)
        w_codes = keep.tile([P, HID_PASSES, D], U32, name="w_codes", align_bytes=64)
        w_scales = keep.tile([P, HID_PASSES, D], U8, name="w_scales", align_bytes=64)
        g_codes = keep.tile([P, BLOCKS, HID_PASSES * P], U32, name="g_codes", align_bytes=64)
        g_scales = keep.tile([P, BLOCKS, HID_PASSES * P], U8, name="g_scales", align_bytes=64)
        make_identity(nc, ident_bf[:])
        make_identity(nc, ident_f32[:])
        b_row = keep.tile([P, D], BF16, name="b_row")
        ones = keep.tile([P, P], BF16, name="ones")
        nc.vector.memset(b_row[:], 0.0)
        nc.vector.memset(ones[:], 1.0)

        tiles = {}

        def ring_tile(tag, key, shape, dtype):
            tiles[key] = sbuf.tile(shape, dtype, name=tag, tag=tag, bufs=RING_BUFS[tag], align_bytes=64)
            return tiles[key]

        def psum_tile(pool, key, shape, dtype):
            tiles[key] = pool.tile(shape, dtype, name="bank", tag="bank")
            return tiles[key]

        def load(what, i, c, queue):
            if what == "k":
                nc.sync.dma_start(
                    out=k_sb[:, PACK * i : PACK * (i + 1), :],
                    in_=k_rows[K_PASS * i : K_PASS * (i + 1), :].rearrange("(p t) d -> p t d", t=PACK),
                )
            elif what == "q":
                nc.sync.dma_start(
                    out=q_sb[:, 4 * i : 4 * i + 4, :],
                    in_=q_rows.rearrange("(p a) d -> p a d", a=BLOCKS)[:, 4 * i : 4 * i + 4, :],
                )
            elif what == "b":
                nc.sync.dma_start(out=b_row[0:1, :], in_=b_out.rearrange("(o d) -> o d", o=1))
            elif what == "v":
                if ("v", i) not in tiles:
                    ring_tile("raw", ("v", i), [P, KEY_PASSES * PACK * K_PASS], BF16)
                view = tiles[("v", i)][:].rearrange("p (c t h) -> p c t h", c=KEY_PASSES, t=PACK)
                nc.sync.dma_start(
                    out=view[:, c, :, :],
                    in_=v_rows[K_PASS * c : K_PASS * (c + 1), K_PASS * i : K_PASS * (i + 1)].rearrange(
                        "(p t) h -> p t h", t=PACK
                    ),
                )
            elif what == "w":
                raw = ring_tile("raw", ("w", i), [P, PACK * 2 * K_PASS], BF16)
                nc.sync.dma_start(
                    out=raw[:].rearrange("p (t h) -> p t h", t=PACK),
                    in_=v_rows[K_PASS * i : K_PASS * (i + 1), 2 * K_PASS :].rearrange("(p t) h -> p t h", t=PACK),
                )
            elif what == "g":
                raw = ring_tile("gate", ("g", i), [P, H], BF16)
                nc.sync.dma_start(out=raw[:], in_=gate_rows[:, i, :])
            elif what == "W":
                raw = ring_tile("raw", ("W", i), [P, 2 * H], BF16)
                nc.sync.dma_start(
                    out=raw[:].rearrange("p (n h) -> p n h", n=2),
                    in_=W_out[2 * P * i : 2 * P * (i + 1), :].rearrange("(n p) h -> p n h", p=P),
                )
            else:
                raw = ring_tile("gate", ("x", i), [P, 2 * D], BF16)
                queue.dma_start(
                    out=raw[:].rearrange("p (a d) -> p a d", a=2), in_=x_rows[:, 2 * i : 2 * i + 2, :]
                )

        def turn_qk(what, half):
            src = k_sb if what == "k" else q_sb
            bank = psum_tile(psum_s, ("T" + what, half), [P, 4, P], BF16)
            for n in range(4):
                nc.tensor.transpose(bank[:, n, :], src[:, 4 * half + n, :], ident_bf[:])

        def keep_qk(what, half, copy):
            dst = kT if what == "k" else qT
            copy(out=dst[:, 4 * half : 4 * half + 4, :], in_=tiles[("T" + what, half)][:])

        def warm_up(n):
            bank = psum_tile(psum_s, ("wu", n), [P, D_HALF], F32)
            nc.tensor.matmul(out=bank[:], lhsT=ones[:], rhs=b_row[:, :D_HALF], start=True, stop=True)

        def spread_bias(half):
            bank = psum_tile(psum_s, ("bb", half), [P, D_HALF], F32)
            cols = slice(D_HALF * half, D_HALF * (half + 1))
            nc.tensor.matmul(out=bank[:], lhsT=ones[:], rhs=b_row[:, cols], start=True, stop=True)

        def keep_bias(half):
            cols = slice(D_HALF * half, D_HALF * (half + 1))
            nc.scalar.copy(out=bias_all[:, cols], in_=tiles[("bb", half)][:])

        def sim(a, c):
            bank = psum_tile(psum_s, ("sc", a, c), [P, PACK, P], F32)
            for t in range(PACK):
                nc.tensor.matmul(
                    out=bank[:, t, :], lhsT=kT[:, PACK * c + t, :], rhs=qT[:, a, :], start=True, stop=True
                )

        def relu(a, c):
            if c == 0:
                ring_tile("relu", ("re", a), [P, KEY_PASSES, P, PACK], F32)
            nc.scalar.activation(
                out=tiles[("re", a)][:, c, :, :],
                in_=tiles[("sc", a, c)][:].rearrange("p t i -> p i t"),
                func=ACT.Relu,
                scale=1.0 / S,
            )

        def square(a):
            grp = ring_tile("a_grp", ("sq", a), [P, KEY_PASSES * P * PACK], BF16)
            nc.scalar.activation(
                out=grp[:], in_=tiles[("re", a)][:].rearrange("p c i t -> p (c i t)"), func=ACT.Square
            )

        def quantise_a(a):
            nc.vector.quantize_mx(
                out=a_codes[:, a, :].bitcast(FP8X4), scales=a_scales[:, a, :], in_=tiles[("sq", a)][:]
            )

        def group_v(g, c, half, copy):
            if ("vg", g, c) not in tiles:
                ring_tile("grp", ("vg", g, c), [P, K_PASS * PACK], BF16)
            if ("w", c) in tiles and g >= 2:
                src = tiles[("w", c)][:].rearrange("p (t e n i) -> p e n t i", t=PACK, e=2, i=4)[:, g - 2, :, :, :]
            else:
                src = tiles[("v", g)][:].rearrange("p (c t n i) -> p c n t i", c=KEY_PASSES, t=PACK, i=4)[:, c, :, :, :]
            dst = tiles[("vg", g, c)][:].rearrange("p (n i t) -> p n t i", i=4, t=PACK)
            rows = slice(64 * half, 64 * half + 64)
            if copy == nc.scalar.copy:
                hop = tiles[("v", g)][:].rearrange("p (c t h) -> p c h t", c=KEY_PASSES, t=PACK)[:, c, :, :]
                cols = slice(256 * half, 256 * half + 256)
                copy(out=tiles[("vg", g, c)][:].rearrange("p (h t) -> p h t", t=PACK)[:, cols, :], in_=hop[:, cols, :])
            else:
                copy(out=dst[:, rows, :, :], in_=src[:, rows, :, :])

        def quantise_v(g, c):
            cols = slice(K_PASS * c, K_PASS * (c + 1))
            nc.vector.quantize_mx(
                out=v_codes[:, g, cols].bitcast(FP8X4), scales=v_scales[:, g, cols], in_=tiles[("vg", g, c)][:]
            )

        def attend(a, g):
            bank = psum_tile(psum_v, ("av", a, g), [P, K_PASS], F32)
            for c in range(KEY_PASSES):
                a_cols = slice(P * c, P * (c + 1))
                v_cols = slice(K_PASS * c, K_PASS * (c + 1))
                nc.tensor.matmul_mx(
                    out=bank[:],
                    lhsT=a_codes[:, a, a_cols].bitcast(FP8X4),
                    lhsT_scale=a_scales[:, a, a_cols],
                    rhs=v_codes[:, g, v_cols].bitcast(FP8X4),
                    rhs_scale=v_scales[:, g, v_cols],
                    start=(c == 0),
                    stop=(c == KEY_PASSES - 1),
                )

        def apply_gate(a, g):
            if g % 2 == 0:
                ring_tile("gated", ("ga", a, g // 2), [P, 2 * K_PASS], BF16)
            cols = slice(K_PASS * (g % 2), K_PASS * (g % 2 + 1))
            nc.vector.tensor_tensor(
                out=tiles[("ga", a, g // 2)][:, cols],
                in0=tiles[("av", a, g)][:],
                in1=tiles[("g", a)][:, K_PASS * g : K_PASS * (g + 1)],
                op=ALU.mult,
            )

        def turn_words(key, words, first_words):
            bank = psum_tile(psum_s, key, [P, 2, 2, P], F32)
            for n in range(2):
                for u in range(2):
                    first = first_words[n] + P * u
                    nc.tensor.transpose(bank[:, n, u, :], words[:, first : first + P], ident_f32[:])

        def turn_v(a, h):
            turn_words(("vt", a, h), tiles[("ga", a, h)][:].bitcast(F32), (0, 2 * P))

        def keep_v(a, h):
            grp = ring_tile("v_t", ("ve", a, h), [P, 2 * K_PASS], BF16)
            nc.scalar.copy(
                out=grp[:].bitcast(F32).rearrange("p (n r u) -> p n r u", n=2, u=2),
                in_=tiles[("vt", a, h)][:].rearrange("p n u r -> p n r u"),
            )

        def quantise_g(a, h):
            cols = slice(2 * P * h, 2 * P * (h + 1))
            nc.vector.quantize_mx(
                out=g_codes[:, a, cols].bitcast(FP8X4), scales=g_scales[:, a, cols], in_=tiles[("ve", a, h)][:]
            )

        def turn_w(g, pair):
            turn_words(("wt", g, pair), tiles[("W", pair)][:].bitcast(F32), [(H // 2) * n + 2 * P * g for n in range(2)])

        def keep_w(g, pair):
            half = pair // 2
            if ("wg", g, half) not in tiles:
                ring_tile("grp", ("wg", g, half), [P, D_HALF * PACK], BF16)
            dst = tiles[("wg", g, half)][:].bitcast(F32).rearrange("p (n r u) -> p n r u", n=4, u=2)
            nc.scalar.copy(
                out=dst[:, 2 * (pair % 2) : 2 * (pair % 2) + 2, :, :],
                in_=tiles[("wt", g, pair)][:].rearrange("p n u r -> p n r u"),
            )

        def quantise_w(g, half):
            cols = slice(D_HALF * half, D_HALF * (half + 1))
            nc.vector.quantize_mx(
                out=w_codes[:, g, cols].bitcast(FP8X4),
                scales=w_scales[:, g, cols],
                in_=tiles[("wg", g, half)][:],
            )

        def residual(a, engine, pieces):
            res = ring_tile("resid", ("rs", a), [P, D], F32)
            for n in range(pieces):
                cols = slice(D // pieces * n, D // pieces * (n + 1))
                x_view = tiles[("x", a // 2)][:].rearrange("p (a d) -> p a d", a=2)
                engine.tensor_tensor(
                    out=res[:, cols], in0=x_view[:, a % 2, cols], in1=bias_all[:, cols], op=ALU.add
                )

        def project(a, half):
            d_cols = slice(D_HALF * half, D_HALF * (half + 1))
            bank = psum_tile(psum_v, ("pj", a, half), [P, D_HALF], F32)
            for g in range(HID_PASSES):
                g_cols = slice(P * g, P * (g + 1))
                nc.tensor.matmul_mx(
                    out=bank[:],
                    lhsT=g_codes[:, a, g_cols].bitcast(FP8X4),
                    lhsT_scale=g_scales[:, a, g_cols],
                    rhs=w_codes[:, g, d_cols].bitcast(FP8X4),
                    rhs_scale=w_scales[:, g, d_cols],
                    start=(g == 0),
                    stop=(g == HID_PASSES - 1),
                )

        def project_piece(a, piece):
            d_cols = slice(D // 4 * piece, D // 4 * (piece + 1))
            bank = psum_tile(psum_v, ("pq", a, piece), [P, D // 4], F32)
            for g in range(HID_PASSES):
                g_cols = slice(P * g, P * (g + 1))
                nc.tensor.matmul_mx(
                    out=bank[:],
                    lhsT=g_codes[:, a, g_cols].bitcast(FP8X4),
                    lhsT_scale=g_scales[:, a, g_cols],
                    rhs=w_codes[:, g, d_cols].bitcast(FP8X4),
                    rhs_scale=w_scales[:, g, d_cols],
                    start=(g == 0),
                    stop=(g == HID_PASSES - 1),
                )

        def finish_piece(a, piece):
            d_cols = slice(D // 4 * piece, D // 4 * (piece + 1))
            res = tiles[("rs", a)]
            nc.vector.tensor_tensor(
                out=res[:, d_cols], in0=tiles[("pq", a, piece)][:], in1=res[:, d_cols], op=ALU.add
            )
            nc.sync.dma_start(out=out_rows[:, a, d_cols], in_=res[:, d_cols])

        def finish(a, half):
            d_cols = slice(D_HALF * half, D_HALF * (half + 1))
            res = tiles[("rs", a)]
            nc.vector.tensor_tensor(
                out=res[:, d_cols], in0=tiles[("pj", a, half)][:], in1=res[:, d_cols], op=ALU.add
            )
            nc.sync.dma_start(out=out_rows[:, a, d_cols], in_=res[:, d_cols])

        def add_residual(a, half):
            d_cols = slice(D_HALF * half, D_HALF * (half + 1))
            if half == 0:
                ring_tile("resid", ("rs", a), [P, D], F32)
            x_view = tiles[("x", a // 2)][:].rearrange("p (a d) -> p a d", a=2)
            nc.vector.tensor_tensor(
                out=tiles[("rs", a)][:, d_cols], in0=tiles[("pj", a, half)][:], in1=x_view[:, a % 2, d_cols], op=ALU.add
            )

        def add_bias(a, half):
            d_cols = slice(D_HALF * half, D_HALF * (half + 1))
            res = tiles[("rs", a)]
            nc.gpsimd.tensor_tensor(out=res[:, d_cols], in0=res[:, d_cols], in1=bias_all[:, d_cols], op=ALU.add)
            nc.sync.dma_start(out=out_rows[:, a, d_cols], in_=res[:, d_cols])

        def task(kind, i, engine):
            copy = nc.scalar.copy if engine == "S" else nc.vector.tensor_copy
            if kind == "ld":
                what, n = i[:2]
                c = i[2] if what == "v" else 0
                buf = {"w": ("raw", 4), "v": ("raw", 4), "W": ("raw", 4), "x": ("gate", 2), "g": ("gate", 4)}
                opens = buf[what] + (("ld", what, n),) if what in buf and ("ld", what, n) not in left else None
                return [], opens, [], lambda: load(what, n, c, nc.scalar if engine == "S" else nc.sync)
            if kind == "T":
                return [("ld",) + i], ("ps", 1, ("T",) + i), [], lambda: turn_qk(*i)
            if kind == "C":
                return [("T",) + i], None, [("T",) + i], lambda: keep_qk(i[0], i[1], copy)
            if kind == "wu":
                return [], ("ps", 0, ("wu",) + i), [], lambda: warm_up(*i)
            if kind == "bb":
                return [("ld", "b", 0)], ("ps", 1, ("bb",) + i), [], lambda: spread_bias(*i)
            if kind == "bk":
                return [("bb",) + i], None, [("bb",) + i], lambda: keep_bias(*i)
            if kind == "sc":
                return [("C", "k", i[1]), ("C", "q", i[0] // 4)], ("ps", 1, ("sc",) + i), [], lambda: sim(*i)
            if kind == "re":
                opens = ("relu", 1, ("re", i[0])) if i[1] == 0 else None
                return [("sc",) + i], opens, [("sc",) + i], lambda: relu(*i)
            if kind == "sq":
                return [("re", i[0], 0), ("re", i[0], 1)], ("a_grp", 1, ("sq",) + i), [("re",) + i], lambda: square(*i)
            if kind == "qA":
                return [("sq",) + i], None, [("sq",) + i], lambda: quantise_a(*i)
            if kind == "vc":
                opens = ("grp", 1, ("vg",) + i[:2]) if ("vg",) + i[:2] not in left else None
                if "ld.w.0" in LOADS and i[0] >= 2:
                    return [("ld", "w", i[1])], opens, [("ld", "w", i[1])], lambda: group_v(i[0], i[1], i[2], copy)
                return [("ld", "v", i[0], i[1])], opens, [("ld", "v", i[0])], lambda: group_v(i[0], i[1], i[2], copy)
            if kind == "qv":
                return [("vc",) + i + (0,), ("vc",) + i + (1,)], None, [("vg",) + i], lambda: quantise_v(*i)
            if kind == "av":
                return [("qA", i[0]), ("qv", i[1], 0), ("qv", i[1], 1)], ("pv", 1, ("av",) + i), [], lambda: attend(*i)
            if kind == "ga":
                opens = ("gated", 1, ("ga", i[0], i[1] // 2)) if i[1] % 2 == 0 else None
                return [("av",) + i, ("ld", "g", i[0])], opens, [("av",) + i, ("ld", "g", i[0])], lambda: apply_gate(*i)
            if kind == "vt":
                a, h = i
                return [("ga", a, 2 * h), ("ga", a, 2 * h + 1)], ("ps", 1, ("vt",) + i), [("ga", a, h)], lambda: turn_v(*i)
            if kind == "ve":
                return [("vt",) + i], ("v_t", 1, ("ve",) + i), [("vt",) + i], lambda: keep_v(*i)
            if kind == "qV":
                return [("ve",) + i], None, [("ve",) + i], lambda: quantise_g(*i)
            if kind == "wt":
                return [("ld", "W", i[1])], ("ps", 1, ("wt",) + i), [("ld", "W", i[1])], lambda: turn_w(*i)
            if kind == "we":
                key = ("wg", i[0], i[1] // 2)
                opens = ("grp", 1, key) if key not in left else None
                return [("wt",) + i], opens, [("wt",) + i], lambda: keep_w(*i)
            if kind == "qW":
                g, h = i
                return [("we", g, 2 * h), ("we", g, 2 * h + 1)], None, [("wg", g, h)], lambda: quantise_w(*i)
            if kind == "rs":
                a = i[0]
                where = (nc.vector, 1) if engine == "V" else (nc.gpsimd, 4)
                needs = [("ld", "x", a // 2), ("bk", 0), ("bk", 1)]
                return needs, ("resid", 2, ("rs", a)), [("ld", "x", a // 2)], lambda: residual(a, *where)
            if kind == "pj":
                a, h = i
                needs = [("qV", a, 0), ("qV", a, 1)] + [("qW", g, h) for g in range(HID_PASSES)]
                return needs, ("pv", 1, ("pj",) + i), [], lambda: project(*i)
            if kind == "pq":
                a, n = i
                needs = [("qV", a, 0), ("qV", a, 1)] + [("qW", g, n // 2) for g in range(HID_PASSES)]
                return needs, ("pv", 1, ("pq",) + i), [], lambda: project_piece(*i)
            if kind == "fq":
                return [("pq",) + i, ("rs", i[0])], None, [("pq",) + i, ("rs", i[0])], lambda: finish_piece(*i)
            if kind == "fx":
                opens = ("resid", 2, ("rs", i[0])) if i[1] == 0 else None
                return [("pj",) + i, ("ld", "x", i[0] // 2)], opens, [("pj",) + i, ("ld", "x", i[0] // 2)], lambda: add_residual(*i)
            if kind == "gb":
                return [("fx",) + i, ("bk", 0), ("bk", 1)], None, [("rs", i[0])], lambda: add_bias(*i)
            return [("pj",) + i, ("rs", i[0])], None, [("pj",) + i, ("rs", i[0])], lambda: finish(*i)

        left = {}
        rings = {name: [] for name in RING_BUFS}
        done = set()
        lanes = []
        for engine, text in (("D", LOADS), ("P", TENSOR), ("S", SCALAR), ("V", VECTOR), ("G", GPSIMD)):
            lane = []
            for word in text.split():
                parts = word.split(".")
                lane.append((parts[0], tuple([n if n in ("k", "q", "v", "w", "W", "g", "b", "x") else int(n) for n in parts[1:]])))
            lanes.append([engine, lane, 0])
        moved = True
        while moved:
            moved = False
            for lane in lanes:
                while lane[2] < len(lane[1]):
                    kind, i = lane[1][lane[2]]
                    needs, opens, reads, call = task(kind, i, lane[0])
                    if not all([n in done for n in needs]):
                        break
                    if opens is not None:
                        held = rings[opens[0]]
                        if len(held) >= RING_BUFS[opens[0]] and left[held[-RING_BUFS[opens[0]]]] > 0:
                            break
                        held.append(opens[2])
                        left[opens[2]] = opens[1]
                    for key in reads:
                        if key in left:
                            left[key] -= 1
                    call()
                    done.add((kind,) + i)
                    lane[2] += 1
                    moved = True
        assert all([lane[2] == len(lane[1]) for lane in lanes]), [lane[1][lane[2]] for lane in lanes if lane[2] < len(lane[1])]
